import numpy as np
import ml_dtypes


def mxq(x, axis, fmt="e4m3"):
    dtype, down = {"e4m3": (ml_dtypes.float8_e4m3fn, 7), "e5m2": (ml_dtypes.float8_e5m2, 14)}[fmt]
    v = np.moveaxis(np.asarray(x, np.float32).astype(ml_dtypes.bfloat16).astype(np.float64), axis, -1)
    blocks = v.reshape(v.shape[:-1] + (-1, 32))
    amax = np.abs(blocks).max(-1, keepdims=True)
    byte = np.maximum(np.where(amax > 0, np.frexp(amax)[1] - 1 + 127, 0) - down, 1)
    scale = np.exp2(byte - 127.0)
    codes = (blocks / scale).astype(np.float32).astype(dtype).astype(np.float64)
    return np.moveaxis((codes * scale).reshape(v.shape), -1, axis)


WIDE = False


def mx_kscale(k):
    if not WIDE:
        return np.ones(k)
    levels = np.array([10, -10, 5, -5, 0])
    a = np.random.permutation(np.resize(levels, k // 512 * 4)).reshape(k // 512, 4)
    idx = np.arange(k)
    return np.exp2(a[idx // 512, idx % 128 // 32])


BF16 = ml_dtypes.bfloat16


def bf(x):
    return np.asarray(x, np.float32).astype(BF16)


def f64(x):
    return np.asarray(x).astype(np.float64)


BATCH, IN_FEATURES, OUT_FEATURES, LOG_DIM = 128, 1024, 512, 10
BUTTERFLY_DIM = 2 ** LOG_DIM
MAX_BLOCKS = BUTTERFLY_DIM // 2


def setup_inputs():
    s = mx_kscale(IN_FEATURES)
    x = np.random.standard_normal((BATCH, IN_FEATURES)) * s
    w_in = np.random.standard_normal((BUTTERFLY_DIM, IN_FEATURES)) / np.sqrt(IN_FEATURES) / s[None, :]
    w_out = np.random.standard_normal((OUT_FEATURES, BUTTERFLY_DIM)) / np.sqrt(BUTTERFLY_DIM)
    b_out = np.random.standard_normal(OUT_FEATURES) * 0.1
    theta = np.random.uniform(0.0, 1.0, (LOG_DIM, MAX_BLOCKS))
    return {"x": bf(x), "w_in": bf(w_in), "w_out": bf(w_out), "b_out": bf(b_out),
            "a_pad": bf(np.cos(theta)), "b_pad": bf(np.sin(theta))}


def _butterfly(x, a_pad, b_pad):
    B = x.shape[0]
    for l in range(LOG_DIM):
        block_size = 2 ** l
        num_blocks = BUTTERFLY_DIM // (2 * block_size)
        a = a_pad[l, :num_blocks][None, :, None]
        b = b_pad[l, :num_blocks][None, :, None]
        xv = x.reshape(B, num_blocks, 2, block_size)
        x0 = xv[:, :, 0, :]
        x1 = xv[:, :, 1, :]
        top = a * x0 + b * x1
        bot = -b * x0 + a * x1
        x = np.stack([top, bot], axis=2).reshape(B, BUTTERFLY_DIM)
    return x


def reference(x, w_in, w_out, b_out, a_pad, b_pad):
    h = mxq(f64(x), 1, "e4m3") @ mxq(f64(w_in), 1, "e4m3").T
    h = _butterfly(h, f64(a_pad), f64(b_pad))
    return (mxq(h, 1, "e4m3") @ mxq(f64(w_out), 1, "e4m3").T) + f64(b_out)

@@ -1,0 +1,296 @@
+from contextlib import ExitStack
+
+import concourse.mybir as mybir
+from concourse.masks import make_identity
+
+F32 = mybir.dt.float32
+BF16 = mybir.dt.bfloat16
+U32 = mybir.dt.uint32
+U8 = mybir.dt.uint8
+FP8X4 = mybir.dt.float8_e4m3fn_x4
+MULT = mybir.AluOpType.mult
+ADD = mybir.AluOpType.add
+COPY = mybir.ActivationFunctionType.Copy
+
+P = 128
+PACK = 4
+K_PASS = P * PACK
+BATCH = 128
+K_IN = 1024
+FEAT = 1024
+N_OUT = 512
+PASSES = K_IN // K_PASS
+HALVES = FEAT // K_PASS
+TABLE = 512
+MID = 7
+FIRST_MID = 2
+LAST = 9
+MIRROR = 32
+COS, NEG_SIN, SIN = 0, 1, 2
+
+FLOPS = 2 * BATCH * K_IN * FEAT + 2 * BATCH * FEAT * N_OUT + 6 * BATCH * (FEAT // 2) * 10
+
+
+def tile_butterflylayer_s_kernel(tc, x, w_in, w_out, b_out, a_pad, b_pad, out):
+    nc = tc.nc
+    with ExitStack() as ctx:
+        keep = ctx.enter_context(tc.tile_pool(name="keep", bufs=1))
+        ring = ctx.enter_context(tc.psum_pool(name="ring", bufs=3))
+        fixed = ctx.enter_context(tc.psum_pool(name="fixed", bufs=1))
+
+        tab_raw = keep.tile([P, 2, TABLE], BF16)
+        nc.vector.memset(tab_raw[:], 0.0)
+        stages = a_pad.shape[0]
+        nc.scalar.dma_start(out=tab_raw[0:stages, 0, :], in_=a_pad)
+        nc.scalar.dma_start(out=tab_raw[0:stages, 1, :], in_=b_pad)
+        nc.scalar.dma_start(out=tab_raw[MIRROR : MIRROR + stages, 0, :], in_=b_pad)
+        nc.scalar.dma_start(out=tab_raw[MIRROR : MIRROR + stages, 1, :], in_=a_pad)
+
+        x_sb = keep.tile([P, K_IN], BF16)
+        nc.sync.dma_start(out=x_sb[:], in_=x)
+        w_sb = keep.tile([P, HALVES, PACK, K_IN], BF16)
+        w_rows = w_in.rearrange("(g p t) k -> p g t k", g=HALVES, t=PACK)
+        for g in range(HALVES):
+            for t in range(0, PACK, 2):
+                nc.sync.dma_start(out=w_sb[:, g, t : t + 2, :], in_=w_rows[:, g, t : t + 2, :])
+        wo_sb = keep.tile([P, PACK, FEAT], BF16)
+        wo_rows = w_out.rearrange("(r c) k -> r c k", c=PACK)
+        for c in range(0, PACK, 2):
+            nc.sync.dma_start(out=wo_sb[:, c : c + 2, :], in_=wo_rows[:, c : c + 2, :])
+
+        ident = keep.tile([P, P], F32)
+        make_identity(nc, ident[:])
+        bias = keep.tile([P, N_OUT], BF16)
+        nc.gpsimd.dma_start(out=bias[:], in_=b_out.partition_broadcast(P))
+
+        def load_k_onto_partitions(word_blocks, grouped):
+            bank = ring.tile([P, 2 * PASSES, P], F32)
+            for b in range(2 * PASSES):
+                nc.tensor.transpose(bank[:, b, :], word_blocks[b], ident[:])
+            nc.scalar.copy(
+                out=grouped.bitcast(F32),
+                in_=bank[:].rearrange("p (c u) r -> p c r u", u=2),
+            )
+
+        def neighbouring_blocks(rows):
+            words = rows.bitcast(F32)
+            return [words[:, b * P : (b + 1) * P] for b in range(2 * PASSES)]
+
+        def alternate_blocks(rows):
+            words = rows.bitcast(F32)
+            half = K_PASS // 2
+            return [
+                words[:, c * half + u : (c + 1) * half : 2] for c in range(PASSES) for u in range(2)
+            ]
+
+        x_grouped = keep.tile([P, PASSES, BATCH, PACK], BF16, align_bytes=64)
+        x_codes = keep.tile([P, PASSES, BATCH], U32, align_bytes=64)
+        x_scales = keep.tile([P, PASSES, BATCH], U8, align_bytes=64)
+        load_k_onto_partitions(neighbouring_blocks(x_sb[:]), x_grouped[:])
+        nc.vector.quantize_mx(
+            out=x_codes[:].rearrange("p c n -> p (c n)").bitcast(FP8X4),
+            scales=x_scales[:].rearrange("p c n -> p (c n)"),
+            in_=x_grouped[:].rearrange("p c n j -> p (c n j)"),
+        )
+
+        sign = keep.tile([P, 1], F32)
+        nc.vector.memset(sign[:], 1.0)
+        nc.vector.memset(sign[MIRROR : 2 * MIRROR, :], -1.0)
+        tab = keep.tile([P, 2, TABLE], BF16)
+        nc.vector.tensor_scalar_mul(out=tab[:, 0, :], in0=tab_raw[:, 0, :], scalar1=sign[:, 0:1])
+        nc.vector.tensor_copy(out=tab[:, 1, :], in_=tab_raw[:, 1, :])
+
+        pick = keep.tile([P, MIRROR, 2], BF16)
+        nc.vector.tensor_copy(out=pick[:], in_=ident[:, 0 : 2 * MIRROR].rearrange("p (e l) -> p l e", e=2))
+
+        def rows_to_columns(dst, src, level):
+            nc.tensor.matmul(out=dst, lhsT=src, rhs=pick[:, level, :], start=True, stop=True)
+
+        coef_ps = fixed.tile([P, 56], F32, tag="small")
+        factor_ps = coef_ps[:, 0:28].rearrange("p (g m e) -> p g m e", g=HALVES, m=MID)
+        rot0_ps = coef_ps[:, 28:44].rearrange("p (g u b e) -> p g u b e", g=HALVES, u=2, b=2)
+        rot1_ps = coef_ps[:, 44:52].rearrange("p (g b e) -> p g b e", g=HALVES, b=2)
+        rot9_ps = coef_ps[:, 52:56].rearrange("p (b e) -> p b e", b=2)
+
+        for b in range(2):
+            for g in range(HALVES):
+                for u in range(2):
+                    first = (TABLE // 2) * g + u
+                    rows_to_columns(rot0_ps[:, g, u, b, :], tab[:, b, first : first + 2 * P - 1 : 2], 0)
+                rows_to_columns(rot1_ps[:, g, b, :], tab[:, b, g * P : (g + 1) * P], 1)
+            rows_to_columns(rot9_ps[:, b, :], tab[:, b, 0:1].to_broadcast([P, P]), LAST)
+
+        spread = keep.tile([P, MID, HALVES * P], BF16)
+        for m in range(MID):
+            entries = P >> m
+            repeat = 1 << m
+            src = tab[:, :, 0:entries].rearrange("p e v -> p v e").unsqueeze(3)
+            src = src.to_broadcast([P, entries, 2, repeat])
+            dst = spread[:, m, :].rearrange("p (v e w) -> p v e w", e=2, w=repeat)
+            if m % 2 == 0:
+                nc.vector.tensor_copy(out=dst, in_=src)
+            else:
+                nc.scalar.copy(out=dst, in_=src)
+            for g in range(HALVES):
+                rows_to_columns(factor_ps[:, g, m, :], spread[:, m, g * P : (g + 1) * P], FIRST_MID + m)
+
+        coef = keep.tile([P, 56], F32)
+        nc.vector.tensor_copy(out=coef[:], in_=coef_ps[:])
+        factor = coef[:, 0:28].rearrange("p (g m e) -> p g m e", g=HALVES, m=MID)
+        rot0 = coef[:, 28:44].rearrange("p (g u c) -> p g u c", g=HALVES, u=2)
+        rot1 = coef[:, 44:52].rearrange("p (g c) -> p g c", g=HALVES)
+        rot9 = coef[:, 52:56]
+
+        mid = factor[:, :, 0, :]
+        for m in range(1, MID):
+            covered = 1 << m
+            wider = keep.tile([P, HALVES, 2 * covered], F32, name="mid%d" % m)
+            nc.vector.tensor_tensor(
+                out=wider[:].rearrange("p g (e w) -> p g e w", e=2),
+                in0=factor[:, :, m, :].unsqueeze(3).to_broadcast([P, HALVES, 2, covered]),
+                in1=mid.unsqueeze(2).to_broadcast([P, HALVES, 2, covered]),
+                op=MULT,
+            )
+            mid = wider[:]
+
+        w_grouped = keep.tile([P, HALVES, PACK, PASSES, P, PACK], BF16, align_bytes=64)
+        w_codes = keep.tile([P, HALVES, PACK, PASSES, P], U32, align_bytes=64)
+        w_scales = keep.tile([P, HALVES, PACK, PASSES, P], U8, align_bytes=64)
+        cos_h = keep.tile([P, HALVES, PACK, BATCH], F32)
+        after0 = keep.tile([P, HALVES, PACK, BATCH], F32)
+        cos_0 = keep.tile([P, HALVES, PACK, BATCH], F32)
+        after1 = keep.tile([P, HALVES, PACK, BATCH], F32)
+        after8 = []
+        for g in range(HALVES):
+            h_ps = fixed.tile([P, PACK, BATCH], F32, name="h%d" % g)
+            for t0 in range(0, PACK, 2):
+                for t in (t0, t0 + 1):
+                    load_k_onto_partitions(neighbouring_blocks(w_sb[:, g, t, :]), w_grouped[:, g, t])
+                nc.vector.quantize_mx(
+                    out=w_codes[:, g, t0 : t0 + 2].rearrange("p t c f -> p (t c f)").bitcast(FP8X4),
+                    scales=w_scales[:, g, t0 : t0 + 2].rearrange("p t c f -> p (t c f)"),
+                    in_=w_grouped[:, g, t0 : t0 + 2].rearrange("p t c f j -> p (t c f j)"),
+                )
+                for t in (t0, t0 + 1):
+                    for c in range(PASSES):
+                        nc.tensor.matmul_mx(
+                            out=h_ps[:, t, :],
+                            lhsT=w_codes[:, g, t, c, :].bitcast(FP8X4),
+                            lhsT_scale=w_scales[:, g, t, c, :],
+                            rhs=x_codes[:, c, :].bitcast(FP8X4),
+                            rhs_scale=x_scales[:, c, :],
+                            start=(c == 0),
+                            stop=(c == PASSES - 1),
+                        )
+
+            for u in range(2):
+                nc.scalar.activation(
+                    out=cos_h[:, g, 2 * u : 2 * u + 2, :],
+                    in_=h_ps[:, 2 * u : 2 * u + 2, :],
+                    func=COPY,
+                    scale=rot0[:, g, u, COS : COS + 1],
+                )
+            for u in (1, 0):
+                nc.vector.scalar_tensor_tensor(
+                    out=after0[:, g, 2 * u, :],
+                    in0=h_ps[:, 2 * u + 1, :],
+                    scalar=rot0[:, g, u, SIN : SIN + 1],
+                    in1=cos_h[:, g, 2 * u, :],
+                    op0=MULT,
+                    op1=ADD,
+                )
+                nc.vector.scalar_tensor_tensor(
+                    out=after0[:, g, 2 * u + 1, :],
+                    in0=h_ps[:, 2 * u, :],
+                    scalar=rot0[:, g, u, NEG_SIN : NEG_SIN + 1],
+                    in1=cos_h[:, g, 2 * u + 1, :],
+                    op0=MULT,
+                    op1=ADD,
+                )
+
+            nc.scalar.activation(
+                out=cos_0[:, g], in_=after0[:, g], func=COPY, scale=rot1[:, g, COS : COS + 1]
+            )
+            nc.vector.scalar_tensor_tensor(
+                out=after1[:, g, 0:2, :],
+                in0=after0[:, g, 2:4, :],
+                scalar=rot1[:, g, SIN : SIN + 1],
+                in1=cos_0[:, g, 0:2, :],
+                op0=MULT,
+                op1=ADD,
+            )
+            nc.vector.scalar_tensor_tensor(
+                out=after1[:, g, 2:4, :],
+                in0=after0[:, g, 0:2, :],
+                scalar=rot1[:, g, NEG_SIN : NEG_SIN + 1],
+                in1=cos_0[:, g, 2:4, :],
+                op0=MULT,
+                op1=ADD,
+            )
+
+            z_ps = fixed.tile([P, PACK, BATCH], F32, name="z%d" % g)
+            nc.tensor.matmul(
+                out=z_ps[:].rearrange("p t n -> p (t n)"),
+                lhsT=mid[:, g, :],
+                rhs=after1[:, g].rearrange("p t n -> p (t n)"),
+                start=True,
+                stop=True,
+            )
+            after8.append(z_ps)
+
+        wo_grouped = keep.tile([P, PASSES, PACK, P, PACK], BF16, align_bytes=64)
+        wo_codes = keep.tile([P, PASSES, PACK, P], U32, align_bytes=64)
+        wo_scales = keep.tile([P, PASSES, PACK, P], U8, align_bytes=64)
+        for c in range(PACK):
+            load_k_onto_partitions(alternate_blocks(wo_sb[:, c, :]), wo_grouped[:, :, c])
+        for g in range(PASSES):
+            nc.vector.quantize_mx(
+                out=wo_codes[:, g].rearrange("p c r -> p (c r)").bitcast(FP8X4),
+                scales=wo_scales[:, g].rearrange("p c r -> p (c r)"),
+                in_=wo_grouped[:, g].rearrange("p c r j -> p (c r j)"),
+            )
+
+        z0 = after8[0][:].rearrange("p t n -> p n t")
+        z1 = after8[1][:].rearrange("p t n -> p n t")
+        from_z0 = keep.tile([P, HALVES, BATCH, PACK], F32)
+        h_grouped = keep.tile([P, HALVES, BATCH, PACK], BF16, align_bytes=64)
+        h_codes = keep.tile([P, HALVES, BATCH], U32, align_bytes=64)
+        h_scales = keep.tile([P, HALVES, BATCH], U8, align_bytes=64)
+        nc.scalar.activation(out=from_z0[:, 0], in_=z0, func=COPY, scale=rot9[:, COS : COS + 1])
+        nc.scalar.activation(out=from_z0[:, 1], in_=z0, func=COPY, scale=rot9[:, NEG_SIN : NEG_SIN + 1])
+        nc.vector.scalar_tensor_tensor(
+            out=h_grouped[:, 0], in0=z1, scalar=rot9[:, SIN : SIN + 1], in1=from_z0[:, 0], op0=MULT, op1=ADD
+        )
+        nc.vector.scalar_tensor_tensor(
+            out=h_grouped[:, 1], in0=z1, scalar=rot9[:, COS : COS + 1], in1=from_z0[:, 1], op0=MULT, op1=ADD
+        )
+        out_ps = fixed.tile([P, PACK, P], F32, tag="small")
+        for g in range(HALVES):
+            nc.vector.quantize_mx(
+                out=h_codes[:, g, :].bitcast(FP8X4),
+                scales=h_scales[:, g, :],
+                in_=h_grouped[:, g].rearrange("p n j -> p (n j)"),
+            )
+        for g in range(HALVES):
+            nc.tensor.matmul_mx(
+                out=out_ps[:].rearrange("p c r -> p (c r)"),
+                lhsT=h_codes[:, g, :].bitcast(FP8X4),
+                lhsT_scale=h_scales[:, g, :],
+                rhs=wo_codes[:, g].rearrange("p c r -> p (c r)").bitcast(FP8X4),
+                rhs_scale=wo_scales[:, g].rearrange("p c r -> p (c r)"),
+                start=(g == 0),
+                stop=(g == HALVES - 1),
+            )
+
+        out_sb = keep.tile([P, P, PACK], F32)
+        bias_rc = bias[:].rearrange("p (r c) -> p r c", c=PACK)
+        out_rc = out.rearrange("n (r c) -> n r c", c=PACK)
+        half = P // 2
+        for r0, queue in ((0, nc.sync), (half, nc.scalar)):
+            nc.vector.tensor_tensor(
+                out=out_sb[:, r0 : r0 + half, :],
+                in0=out_ps[:, :, r0 : r0 + half].rearrange("p c r -> p r c"),
+                in1=bias_rc[:, r0 : r0 + half, :],
+                op=ADD,
+            )
+            queue.dma_start(out=out_rc[:, r0 : r0 + half, :], in_=out_sb[:, r0 : r0 + half, :])

@@ -57,11 +57,11 @@ def tile_butterflylayer_s_kernel(tc, x, w_in, w_out, b_out, a_pad, b_pad, out):
         wo_rows = w_out.rearrange("(r c) k -> r c k", c=PACK)
         for c in range(0, PACK, 2):
             nc.sync.dma_start(out=wo_sb[:, c : c + 2, :], in_=wo_rows[:, c : c + 2, :])
+        bias = keep.tile([P, N_OUT], BF16)
+        nc.sync.dma_start(out=bias[:], in_=b_out.partition_broadcast(P))
 
         ident = keep.tile([P, P], F32)
         make_identity(nc, ident[:])
-        bias = keep.tile([P, N_OUT], BF16)
-        nc.gpsimd.dma_start(out=bias[:], in_=b_out.partition_broadcast(P))
 
         def load_k_onto_partitions(word_blocks, grouped):
             bank = ring.tile([P, 2 * PASSES, P], F32)

@@ -7,6 +7,7 @@ F32 = mybir.dt.float32
 BF16 = mybir.dt.bfloat16
 U32 = mybir.dt.uint32
 U8 = mybir.dt.uint8
+I32 = mybir.dt.int32
 FP8X4 = mybir.dt.float8_e4m3fn_x4
 MULT = mybir.AluOpType.mult
 ADD = mybir.AluOpType.add
@@ -27,6 +28,8 @@ FIRST_MID = 2
 LAST = 9
 MIRROR = 32
 COS, NEG_SIN, SIN = 0, 1, 2
+ROT1 = 4
+ROT9 = 6
 
 FLOPS = 2 * BATCH * K_IN * FEAT + 2 * BATCH * FEAT * N_OUT + 6 * BATCH * (FEAT // 2) * 10
 
@@ -35,26 +38,33 @@ def tile_butterflylayer_s_kernel(tc, x, w_in, w_out, b_out, a_pad, b_pad, out):
     nc = tc.nc
     with ExitStack() as ctx:
         keep = ctx.enter_context(tc.tile_pool(name="keep", bufs=1))
-        ring = ctx.enter_context(tc.psum_pool(name="ring", bufs=3))
+        ring = ctx.enter_context(tc.psum_pool(name="ring", bufs=4))
         fixed = ctx.enter_context(tc.psum_pool(name="fixed", bufs=1))
+        ctx.enter_context(tc.manual_schedule())
 
-        tab_raw = keep.tile([P, 2, TABLE], BF16)
-        nc.vector.memset(tab_raw[:], 0.0)
-        stages = a_pad.shape[0]
-        nc.scalar.dma_start(out=tab_raw[0:stages, 0, :], in_=a_pad)
-        nc.scalar.dma_start(out=tab_raw[0:stages, 1, :], in_=b_pad)
-        nc.scalar.dma_start(out=tab_raw[MIRROR : MIRROR + stages, 0, :], in_=b_pad)
-        nc.scalar.dma_start(out=tab_raw[MIRROR : MIRROR + stages, 1, :], in_=a_pad)
+        tab = keep.tile([P, 2, TABLE], BF16)
+        nc.vector.memset(tab[:].bitcast(I32), 0)
+        sign = keep.tile([P, 1], F32)
+        nc.vector.memset(sign[:], 1.0)
+        nc.vector.memset(sign[MIRROR : 2 * MIRROR, :], -1.0)
+        factor = keep.tile([P, HALVES, MID + 1, 2], F32)
+        nc.vector.memset(factor[:], 1.0)
 
         x_sb = keep.tile([P, K_IN], BF16)
         nc.sync.dma_start(out=x_sb[:], in_=x)
+        stages = a_pad.shape[0]
+        nc.sync.dma_start(out=tab[0:stages, 0, :], in_=a_pad)
+        nc.sync.dma_start(out=tab[0:stages, 1, :], in_=b_pad)
+        nc.sync.dma_start(out=tab[MIRROR : MIRROR + stages, 0, :], in_=b_pad)
+        nc.sync.dma_start(out=tab[MIRROR : MIRROR + stages, 1, :], in_=a_pad)
+
         w_sb = keep.tile([P, HALVES, PACK, K_IN], BF16)
         w_rows = w_in.rearrange("(g p t) k -> p g t k", g=HALVES, t=PACK)
         for g in range(HALVES):
             for t in range(0, PACK, 2):
                 nc.sync.dma_start(out=w_sb[:, g, t : t + 2, :], in_=w_rows[:, g, t : t + 2, :])
         wo_sb = keep.tile([P, PACK, FEAT], BF16)
-        wo_rows = w_out.rearrange("(r c) k -> r c k", c=PACK)
+        wo_rows = w_out.rearrange("(c r) k -> r c k", c=PACK)
         for c in range(0, PACK, 2):
             nc.sync.dma_start(out=wo_sb[:, c : c + 2, :], in_=wo_rows[:, c : c + 2, :])
         bias = keep.tile([P, N_OUT], BF16)
@@ -62,15 +72,6 @@ def tile_butterflylayer_s_kernel(tc, x, w_in, w_out, b_out, a_pad, b_pad, out):
 
         ident = keep.tile([P, P], F32)
         make_identity(nc, ident[:])
-
-        def load_k_onto_partitions(word_blocks, grouped):
-            bank = ring.tile([P, 2 * PASSES, P], F32)
-            for b in range(2 * PASSES):
-                nc.tensor.transpose(bank[:, b, :], word_blocks[b], ident[:])
-            nc.scalar.copy(
-                out=grouped.bitcast(F32),
-                in_=bank[:].rearrange("p (c u) r -> p c r u", u=2),
-            )
 
         def neighbouring_blocks(rows):
             words = rows.bitcast(F32)
@@ -83,22 +84,23 @@ def tile_butterflylayer_s_kernel(tc, x, w_in, w_out, b_out, a_pad, b_pad, out):
                 words[:, c * half + u : (c + 1) * half : 2] for c in range(PASSES) for u in range(2)
             ]
 
-        x_grouped = keep.tile([P, PASSES, BATCH, PACK], BF16, align_bytes=64)
-        x_codes = keep.tile([P, PASSES, BATCH], U32, align_bytes=64)
-        x_scales = keep.tile([P, PASSES, BATCH], U8, align_bytes=64)
-        load_k_onto_partitions(neighbouring_blocks(x_sb[:]), x_grouped[:])
-        nc.vector.quantize_mx(
-            out=x_codes[:].rearrange("p c n -> p (c n)").bitcast(FP8X4),
-            scales=x_scales[:].rearrange("p c n -> p (c n)"),
-            in_=x_grouped[:].rearrange("p c n j -> p (c n j)"),
-        )
+        def transpose_chunk(word_blocks):
+            bank = ring.tile([P, 2 * PASSES, P], F32, name="bank")
+            for b in range(2 * PASSES):
+                nc.tensor.transpose(bank[:, b, :], word_blocks[b], ident[:])
+            return bank
 
-        sign = keep.tile([P, 1], F32)
-        nc.vector.memset(sign[:], 1.0)
-        nc.vector.memset(sign[MIRROR : 2 * MIRROR, :], -1.0)
-        tab = keep.tile([P, 2, TABLE], BF16)
-        nc.vector.tensor_scalar_mul(out=tab[:, 0, :], in0=tab_raw[:, 0, :], scalar1=sign[:, 0:1])
-        nc.vector.tensor_copy(out=tab[:, 1, :], in_=tab_raw[:, 1, :])
+        def regroup_chunk(bank, grouped):
+            nc.scalar.copy(
+                out=grouped.bitcast(F32), in_=bank[:].rearrange("p (c u) r -> p c r u", u=2)
+            )
+
+        def quantise_chunk(grouped, codes, scales):
+            nc.vector.quantize_mx(
+                out=codes.rearrange("p c r -> p (c r)").bitcast(FP8X4),
+                scales=scales.rearrange("p c r -> p (c r)"),
+                in_=grouped.rearrange("p c r j -> p (c r j)"),
+            )
 
         pick = keep.tile([P, MIRROR, 2], BF16)
         nc.vector.tensor_copy(out=pick[:], in_=ident[:, 0 : 2 * MIRROR].rearrange("p (e l) -> p l e", e=2))
@@ -106,191 +108,192 @@ def tile_butterflylayer_s_kernel(tc, x, w_in, w_out, b_out, a_pad, b_pad, out):
         def rows_to_columns(dst, src, level):
             nc.tensor.matmul(out=dst, lhsT=src, rhs=pick[:, level, :], start=True, stop=True)
 
-        coef_ps = fixed.tile([P, 56], F32, tag="small")
-        factor_ps = coef_ps[:, 0:28].rearrange("p (g m e) -> p g m e", g=HALVES, m=MID)
-        rot0_ps = coef_ps[:, 28:44].rearrange("p (g u b e) -> p g u b e", g=HALVES, u=2, b=2)
-        rot1_ps = coef_ps[:, 44:52].rearrange("p (g b e) -> p g b e", g=HALVES, b=2)
-        rot9_ps = coef_ps[:, 52:56].rearrange("p (b e) -> p b e", b=2)
-
-        for b in range(2):
-            for g in range(HALVES):
-                for u in range(2):
-                    first = (TABLE // 2) * g + u
-                    rows_to_columns(rot0_ps[:, g, u, b, :], tab[:, b, first : first + 2 * P - 1 : 2], 0)
-                rows_to_columns(rot1_ps[:, g, b, :], tab[:, b, g * P : (g + 1) * P], 1)
-            rows_to_columns(rot9_ps[:, b, :], tab[:, b, 0:1].to_broadcast([P, P]), LAST)
+        nc.vector.tensor_scalar_mul(out=tab[:, 0, :], in0=tab[:, 0, :], scalar1=sign[:, 0:1])
 
         spread = keep.tile([P, MID, HALVES * P], BF16)
         for m in range(MID):
             entries = P >> m
             repeat = 1 << m
             src = tab[:, :, 0:entries].rearrange("p e v -> p v e").unsqueeze(3)
-            src = src.to_broadcast([P, entries, 2, repeat])
-            dst = spread[:, m, :].rearrange("p (v e w) -> p v e w", e=2, w=repeat)
-            if m % 2 == 0:
-                nc.vector.tensor_copy(out=dst, in_=src)
-            else:
-                nc.scalar.copy(out=dst, in_=src)
-            for g in range(HALVES):
-                rows_to_columns(factor_ps[:, g, m, :], spread[:, m, g * P : (g + 1) * P], FIRST_MID + m)
-
-        coef = keep.tile([P, 56], F32)
-        nc.vector.tensor_copy(out=coef[:], in_=coef_ps[:])
-        factor = coef[:, 0:28].rearrange("p (g m e) -> p g m e", g=HALVES, m=MID)
-        rot0 = coef[:, 28:44].rearrange("p (g u c) -> p g u c", g=HALVES, u=2)
-        rot1 = coef[:, 44:52].rearrange("p (g c) -> p g c", g=HALVES)
-        rot9 = coef[:, 52:56]
-
-        mid = factor[:, :, 0, :]
-        for m in range(1, MID):
-            covered = 1 << m
-            wider = keep.tile([P, HALVES, 2 * covered], F32, name="mid%d" % m)
-            nc.vector.tensor_tensor(
-                out=wider[:].rearrange("p g (e w) -> p g e w", e=2),
-                in0=factor[:, :, m, :].unsqueeze(3).to_broadcast([P, HALVES, 2, covered]),
-                in1=mid.unsqueeze(2).to_broadcast([P, HALVES, 2, covered]),
-                op=MULT,
+            nc.gpsimd.tensor_scalar(
+                out=spread[:, m, :].rearrange("p (v e w) -> p v e w", e=2, w=repeat),
+                in0=src.to_broadcast([P, entries, 2, repeat]),
+                scalar1=1.0,
+                scalar2=0.0,
+                op0=MULT,
+                op1=ADD,
             )
-            mid = wider[:]
+
+        x_grouped = keep.tile([P, PASSES, BATCH, PACK], BF16, align_bytes=64)
+        x_codes = keep.tile([P, PASSES, BATCH], U32, align_bytes=64)
+        x_scales = keep.tile([P, PASSES, BATCH], U8, align_bytes=64)
+        regroup_chunk(transpose_chunk(neighbouring_blocks(x_sb[:])), x_grouped[:])
+
+        rot_ps = fixed.tile([P, ROT9 + 1, 2], F32, name="rot_ps", tag="z0")
+        for g in range(HALVES):
+            for u in range(2):
+                first = (TABLE // 2) * g + u
+                rows_to_columns(rot_ps[:, 2 * g + u, :], tab[:, 0, first : first + 2 * P - 1 : 2], 0)
+            rows_to_columns(rot_ps[:, ROT1 + g, :], tab[:, 0, g * P : (g + 1) * P], 1)
+        rows_to_columns(rot_ps[:, ROT9, :], tab[:, 0, 0:1].to_broadcast([P, P]), LAST)
+
+        quantise_chunk(x_grouped[:], x_codes[:], x_scales[:])
+        rot = keep.tile([P, ROT9 + 1, 3], F32)
+        nc.vector.tensor_copy(out=rot[:, :, COS : NEG_SIN + 1], in_=rot_ps[:])
+        nc.vector.tensor_scalar_mul(out=rot[:, :, SIN], in0=rot[:, :, NEG_SIN], scalar1=-1.0)
+
+        def build_mid():
+            factor_ps = fixed.tile([P, HALVES, MID, 2], F32, name="factor_ps", tag="z1")
+            for m in range(MID):
+                for g in range(HALVES):
+                    rows_to_columns(factor_ps[:, g, m, :], spread[:, m, g * P : (g + 1) * P], FIRST_MID + m)
+            nc.vector.tensor_copy(out=factor[:, :, 0:MID, :], in_=factor_ps[:])
+
+            def outer(groups, high, low, tables):
+                wider = keep.tile([P, groups, high, low], F32, name="outer%d" % low)
+                two = tables.rearrange("p (k two) w -> p k two w", two=2)
+                nc.vector.tensor_tensor(
+                    out=wider[:],
+                    in0=two[:, :, 1, 0:high].unsqueeze(3).to_broadcast([P, groups, high, low]),
+                    in1=two[:, :, 0, :].unsqueeze(2).to_broadcast([P, groups, high, low]),
+                    op=MULT,
+                )
+                return wider[:].rearrange("p k a b -> p k (a b)")
+
+            bits2 = outer(4 * HALVES, 2, 2, factor[:].rearrange("p g m e -> p (g m) e"))
+            bits4 = outer(2 * HALVES, 4, 4, bits2)
+            return outer(HALVES, 8, 16, bits4)
 
         w_grouped = keep.tile([P, HALVES, PACK, PASSES, P, PACK], BF16, align_bytes=64)
         w_codes = keep.tile([P, HALVES, PACK, PASSES, P], U32, align_bytes=64)
         w_scales = keep.tile([P, HALVES, PACK, PASSES, P], U8, align_bytes=64)
+        h_ps = [fixed.tile([P, PACK, BATCH], F32, name="h%d" % g, tag="h%d" % g) for g in range(HALVES)]
+
+        def prepare(g, t0):
+            for t in (t0, t0 + 1):
+                regroup_chunk(transpose_chunk(neighbouring_blocks(w_sb[:, g, t, :])), w_grouped[:, g, t])
+                quantise_chunk(w_grouped[:, g, t], w_codes[:, g, t], w_scales[:, g, t])
+
+        def multiply(g, t0):
+            for t in (t0, t0 + 1):
+                for c in range(PASSES):
+                    nc.tensor.matmul_mx(
+                        out=h_ps[g][:, t, :],
+                        lhsT=w_codes[:, g, t, c, :].bitcast(FP8X4),
+                        lhsT_scale=w_scales[:, g, t, c, :],
+                        rhs=x_codes[:, c, :].bitcast(FP8X4),
+                        rhs_scale=x_scales[:, c, :],
+                        start=(c == 0),
+                        stop=(c == PASSES - 1),
+                    )
+
+        prepare(0, 0)
+        prepare(0, 2)
+        multiply(0, 0)
+        mid = build_mid()
+        prepare(1, 0)
+        multiply(0, 2)
+        prepare(1, 2)
+        multiply(1, 0)
+        multiply(1, 2)
+
+        wo_banks = [transpose_chunk(alternate_blocks(wo_sb[:, c, :])) for c in range(PACK)]
+
+        def rotate(dst, src, cos_src, first, second, which):
+            for mine, partner, sine in ((second, first, NEG_SIN), (first, second, SIN)):
+                nc.vector.scalar_tensor_tensor(
+                    out=dst[:, mine, :],
+                    in0=src[:, partner, :],
+                    scalar=rot[:, which, sine : sine + 1],
+                    in1=cos_src[:, mine, :],
+                    op0=MULT,
+                    op1=ADD,
+                )
+
         cos_h = keep.tile([P, HALVES, PACK, BATCH], F32)
         after0 = keep.tile([P, HALVES, PACK, BATCH], F32)
         cos_0 = keep.tile([P, HALVES, PACK, BATCH], F32)
         after1 = keep.tile([P, HALVES, PACK, BATCH], F32)
-        after8 = []
         for g in range(HALVES):
-            h_ps = fixed.tile([P, PACK, BATCH], F32, name="h%d" % g)
-            for t0 in range(0, PACK, 2):
-                for t in (t0, t0 + 1):
-                    load_k_onto_partitions(neighbouring_blocks(w_sb[:, g, t, :]), w_grouped[:, g, t])
-                nc.vector.quantize_mx(
-                    out=w_codes[:, g, t0 : t0 + 2].rearrange("p t c f -> p (t c f)").bitcast(FP8X4),
-                    scales=w_scales[:, g, t0 : t0 + 2].rearrange("p t c f -> p (t c f)"),
-                    in_=w_grouped[:, g, t0 : t0 + 2].rearrange("p t c f j -> p (t c f j)"),
-                )
-                for t in (t0, t0 + 1):
-                    for c in range(PASSES):
-                        nc.tensor.matmul_mx(
-                            out=h_ps[:, t, :],
-                            lhsT=w_codes[:, g, t, c, :].bitcast(FP8X4),
-                            lhsT_scale=w_scales[:, g, t, c, :],
-                            rhs=x_codes[:, c, :].bitcast(FP8X4),
-                            rhs_scale=x_scales[:, c, :],
-                            start=(c == 0),
-                            stop=(c == PASSES - 1),
-                        )
-
             for u in range(2):
                 nc.scalar.activation(
                     out=cos_h[:, g, 2 * u : 2 * u + 2, :],
-                    in_=h_ps[:, 2 * u : 2 * u + 2, :],
+                    in_=h_ps[g][:, 2 * u : 2 * u + 2, :],
                     func=COPY,
-                    scale=rot0[:, g, u, COS : COS + 1],
+                    scale=rot[:, 2 * g + u, COS : COS + 1],
                 )
             for u in (1, 0):
-                nc.vector.scalar_tensor_tensor(
-                    out=after0[:, g, 2 * u, :],
-                    in0=h_ps[:, 2 * u + 1, :],
-                    scalar=rot0[:, g, u, SIN : SIN + 1],
-                    in1=cos_h[:, g, 2 * u, :],
-                    op0=MULT,
-                    op1=ADD,
-                )
-                nc.vector.scalar_tensor_tensor(
-                    out=after0[:, g, 2 * u + 1, :],
-                    in0=h_ps[:, 2 * u, :],
-                    scalar=rot0[:, g, u, NEG_SIN : NEG_SIN + 1],
-                    in1=cos_h[:, g, 2 * u + 1, :],
-                    op0=MULT,
-                    op1=ADD,
-                )
-
+                rotate(after0[:, g], h_ps[g], cos_h[:, g], 2 * u, 2 * u + 1, 2 * g + u)
+        for g in range(HALVES):
             nc.scalar.activation(
-                out=cos_0[:, g], in_=after0[:, g], func=COPY, scale=rot1[:, g, COS : COS + 1]
+                out=cos_0[:, g], in_=after0[:, g], func=COPY, scale=rot[:, ROT1 + g, COS : COS + 1]
             )
-            nc.vector.scalar_tensor_tensor(
-                out=after1[:, g, 0:2, :],
-                in0=after0[:, g, 2:4, :],
-                scalar=rot1[:, g, SIN : SIN + 1],
-                in1=cos_0[:, g, 0:2, :],
-                op0=MULT,
-                op1=ADD,
-            )
-            nc.vector.scalar_tensor_tensor(
-                out=after1[:, g, 2:4, :],
-                in0=after0[:, g, 0:2, :],
-                scalar=rot1[:, g, NEG_SIN : NEG_SIN + 1],
-                in1=cos_0[:, g, 2:4, :],
-                op0=MULT,
-                op1=ADD,
-            )
+            rotate(after1[:, g], after0[:, g], cos_0[:, g], slice(0, 2), slice(2, 4), ROT1 + g)
 
-            z_ps = fixed.tile([P, PACK, BATCH], F32, name="z%d" % g)
+        z_ps = [fixed.tile([P, PACK, BATCH], F32, name="z%d" % g, tag="z%d" % g) for g in range(HALVES)]
+        for g in range(HALVES):
             nc.tensor.matmul(
-                out=z_ps[:].rearrange("p t n -> p (t n)"),
+                out=z_ps[g][:].rearrange("p t n -> p (t n)"),
                 lhsT=mid[:, g, :],
                 rhs=after1[:, g].rearrange("p t n -> p (t n)"),
                 start=True,
                 stop=True,
             )
-            after8.append(z_ps)
 
-        wo_grouped = keep.tile([P, PASSES, PACK, P, PACK], BF16, align_bytes=64)
-        wo_codes = keep.tile([P, PASSES, PACK, P], U32, align_bytes=64)
-        wo_scales = keep.tile([P, PASSES, PACK, P], U8, align_bytes=64)
-        for c in range(PACK):
-            load_k_onto_partitions(alternate_blocks(wo_sb[:, c, :]), wo_grouped[:, :, c])
-        for g in range(PASSES):
-            nc.vector.quantize_mx(
-                out=wo_codes[:, g].rearrange("p c r -> p (c r)").bitcast(FP8X4),
-                scales=wo_scales[:, g].rearrange("p c r -> p (c r)"),
-                in_=wo_grouped[:, g].rearrange("p c r j -> p (c r j)"),
-            )
+        wo_grouped = keep.tile([P, PACK, PASSES, P, PACK], BF16, align_bytes=64)
+        wo_codes = keep.tile([P, PACK, PASSES, P], U32, align_bytes=64)
+        wo_scales = keep.tile([P, PACK, PASSES, P], U8, align_bytes=64)
+        for c in (0, 1):
+            regroup_chunk(wo_banks[c], wo_grouped[:, c])
+            quantise_chunk(wo_grouped[:, c], wo_codes[:, c], wo_scales[:, c])
 
-        z0 = after8[0][:].rearrange("p t n -> p n t")
-        z1 = after8[1][:].rearrange("p t n -> p n t")
+        z0 = z_ps[0][:].rearrange("p t n -> p n t")
+        z1 = z_ps[1][:].rearrange("p t n -> p n t")
         from_z0 = keep.tile([P, HALVES, BATCH, PACK], F32)
         h_grouped = keep.tile([P, HALVES, BATCH, PACK], BF16, align_bytes=64)
         h_codes = keep.tile([P, HALVES, BATCH], U32, align_bytes=64)
         h_scales = keep.tile([P, HALVES, BATCH], U8, align_bytes=64)
-        nc.scalar.activation(out=from_z0[:, 0], in_=z0, func=COPY, scale=rot9[:, COS : COS + 1])
-        nc.scalar.activation(out=from_z0[:, 1], in_=z0, func=COPY, scale=rot9[:, NEG_SIN : NEG_SIN + 1])
-        nc.vector.scalar_tensor_tensor(
-            out=h_grouped[:, 0], in0=z1, scalar=rot9[:, SIN : SIN + 1], in1=from_z0[:, 0], op0=MULT, op1=ADD
-        )
-        nc.vector.scalar_tensor_tensor(
-            out=h_grouped[:, 1], in0=z1, scalar=rot9[:, COS : COS + 1], in1=from_z0[:, 1], op0=MULT, op1=ADD
-        )
-        out_ps = fixed.tile([P, PACK, P], F32, tag="small")
+        for g, of_z0, of_z1 in ((0, COS, SIN), (1, NEG_SIN, COS)):
+            nc.scalar.activation(
+                out=from_z0[:, g], in_=z0, func=COPY, scale=rot[:, ROT9, of_z0 : of_z0 + 1]
+            )
+            nc.vector.scalar_tensor_tensor(
+                out=h_grouped[:, g],
+                in0=z1,
+                scalar=rot[:, ROT9, of_z1 : of_z1 + 1],
+                in1=from_z0[:, g],
+                op0=MULT,
+                op1=ADD,
+            )
         for g in range(HALVES):
             nc.vector.quantize_mx(
                 out=h_codes[:, g, :].bitcast(FP8X4),
                 scales=h_scales[:, g, :],
                 in_=h_grouped[:, g].rearrange("p n j -> p (n j)"),
             )
-        for g in range(HALVES):
-            nc.tensor.matmul_mx(
-                out=out_ps[:].rearrange("p c r -> p (c r)"),
-                lhsT=h_codes[:, g, :].bitcast(FP8X4),
-                lhsT_scale=h_scales[:, g, :],
-                rhs=wo_codes[:, g].rearrange("p c r -> p (c r)").bitcast(FP8X4),
-                rhs_scale=wo_scales[:, g].rearrange("p c r -> p (c r)"),
-                start=(g == 0),
-                stop=(g == HALVES - 1),
-            )
+        for c in (2, 3):
+            regroup_chunk(wo_banks[c], wo_grouped[:, c])
+            quantise_chunk(wo_grouped[:, c], wo_codes[:, c], wo_scales[:, c])
 
-        out_sb = keep.tile([P, P, PACK], F32)
-        bias_rc = bias[:].rearrange("p (r c) -> p r c", c=PACK)
-        out_rc = out.rearrange("n (r c) -> n r c", c=PACK)
-        half = P // 2
-        for r0, queue in ((0, nc.sync), (half, nc.scalar)):
-            nc.vector.tensor_tensor(
-                out=out_sb[:, r0 : r0 + half, :],
-                in0=out_ps[:, :, r0 : r0 + half].rearrange("p c r -> p r c"),
-                in1=bias_rc[:, r0 : r0 + half, :],
-                op=ADD,
-            )
-            queue.dma_start(out=out_rc[:, r0 : r0 + half, :], in_=out_sb[:, r0 : r0 + half, :])
+        out_ps = [fixed.tile([P, 2, P], F32, name="out_ps%d" % b, tag="h%d" % b) for b in range(2)]
+        out_sb = keep.tile([P, N_OUT], F32)
+        for c in range(PACK):
+            for g in range(HALVES):
+                nc.tensor.matmul_mx(
+                    out=out_ps[c // 2][:, c % 2, :],
+                    lhsT=h_codes[:, g, :].bitcast(FP8X4),
+                    lhsT_scale=h_scales[:, g, :],
+                    rhs=wo_codes[:, c, g, :].bitcast(FP8X4),
+                    rhs_scale=wo_scales[:, c, g, :],
+                    start=(g == 0),
+                    stop=(g == HALVES - 1),
+                )
+            if c % 2 == 1:
+                cols = slice((c - 1) * P, (c + 1) * P)
+                nc.vector.tensor_tensor(
+                    out=out_sb[:, cols],
+                    in0=out_ps[c // 2][:].rearrange("p c r -> p (c r)"),
+                    in1=bias[:, cols],
+                    op=ADD,
+                )
+                nc.sync.dma_start(out=out[:, cols], in_=out_sb[:, cols])

@@ -53,10 +53,10 @@ def tile_butterflylayer_s_kernel(tc, x, w_in, w_out, b_out, a_pad, b_pad, out):
         x_sb = keep.tile([P, K_IN], BF16)
         nc.sync.dma_start(out=x_sb[:], in_=x)
         stages = a_pad.shape[0]
-        nc.sync.dma_start(out=tab[0:stages, 0, :], in_=a_pad)
-        nc.sync.dma_start(out=tab[0:stages, 1, :], in_=b_pad)
-        nc.sync.dma_start(out=tab[MIRROR : MIRROR + stages, 0, :], in_=b_pad)
-        nc.sync.dma_start(out=tab[MIRROR : MIRROR + stages, 1, :], in_=a_pad)
+        nc.scalar.dma_start(out=tab[0:stages, 0, :], in_=a_pad)
+        nc.scalar.dma_start(out=tab[0:stages, 1, :], in_=b_pad)
+        nc.scalar.dma_start(out=tab[MIRROR : MIRROR + stages, 0, :], in_=b_pad)
+        nc.scalar.dma_start(out=tab[MIRROR : MIRROR + stages, 1, :], in_=a_pad)
 
         w_sb = keep.tile([P, HALVES, PACK, K_IN], BF16)
         w_rows = w_in.rearrange("(g p t) k -> p g t k", g=HALVES, t=PACK)
@@ -127,118 +127,133 @@ def tile_butterflylayer_s_kernel(tc, x, w_in, w_out, b_out, a_pad, b_pad, out):
         x_grouped = keep.tile([P, PASSES, BATCH, PACK], BF16, align_bytes=64)
         x_codes = keep.tile([P, PASSES, BATCH], U32, align_bytes=64)
         x_scales = keep.tile([P, PASSES, BATCH], U8, align_bytes=64)
-        regroup_chunk(transpose_chunk(neighbouring_blocks(x_sb[:])), x_grouped[:])
-
-        rot_ps = fixed.tile([P, ROT9 + 1, 2], F32, name="rot_ps", tag="z0")
-        for g in range(HALVES):
-            for u in range(2):
-                first = (TABLE // 2) * g + u
-                rows_to_columns(rot_ps[:, 2 * g + u, :], tab[:, 0, first : first + 2 * P - 1 : 2], 0)
-            rows_to_columns(rot_ps[:, ROT1 + g, :], tab[:, 0, g * P : (g + 1) * P], 1)
-        rows_to_columns(rot_ps[:, ROT9, :], tab[:, 0, 0:1].to_broadcast([P, P]), LAST)
-
-        quantise_chunk(x_grouped[:], x_codes[:], x_scales[:])
-        rot = keep.tile([P, ROT9 + 1, 3], F32)
-        nc.vector.tensor_copy(out=rot[:, :, COS : NEG_SIN + 1], in_=rot_ps[:])
-        nc.vector.tensor_scalar_mul(out=rot[:, :, SIN], in0=rot[:, :, NEG_SIN], scalar1=-1.0)
-
-        def build_mid():
-            factor_ps = fixed.tile([P, HALVES, MID, 2], F32, name="factor_ps", tag="z1")
-            for m in range(MID):
-                for g in range(HALVES):
-                    rows_to_columns(factor_ps[:, g, m, :], spread[:, m, g * P : (g + 1) * P], FIRST_MID + m)
-            nc.vector.tensor_copy(out=factor[:, :, 0:MID, :], in_=factor_ps[:])
-
-            def outer(groups, high, low, tables):
-                wider = keep.tile([P, groups, high, low], F32, name="outer%d" % low)
-                two = tables.rearrange("p (k two) w -> p k two w", two=2)
-                nc.vector.tensor_tensor(
-                    out=wider[:],
-                    in0=two[:, :, 1, 0:high].unsqueeze(3).to_broadcast([P, groups, high, low]),
-                    in1=two[:, :, 0, :].unsqueeze(2).to_broadcast([P, groups, high, low]),
-                    op=MULT,
-                )
-                return wider[:].rearrange("p k a b -> p k (a b)")
-
-            bits2 = outer(4 * HALVES, 2, 2, factor[:].rearrange("p g m e -> p (g m) e"))
-            bits4 = outer(2 * HALVES, 4, 4, bits2)
-            return outer(HALVES, 8, 16, bits4)
-
         w_grouped = keep.tile([P, HALVES, PACK, PASSES, P, PACK], BF16, align_bytes=64)
         w_codes = keep.tile([P, HALVES, PACK, PASSES, P], U32, align_bytes=64)
         w_scales = keep.tile([P, HALVES, PACK, PASSES, P], U8, align_bytes=64)
-        h_ps = [fixed.tile([P, PACK, BATCH], F32, name="h%d" % g, tag="h%d" % g) for g in range(HALVES)]
+        h_ps = [
+            fixed.tile([P, 2, BATCH], F32, name="h%d" % piece, tag="piece%d" % piece)
+            for piece in range(2 * HALVES)
+        ]
 
-        def prepare(g, t0):
-            for t in (t0, t0 + 1):
+        def prepare(g, u):
+            for t in (2 * u, 2 * u + 1):
                 regroup_chunk(transpose_chunk(neighbouring_blocks(w_sb[:, g, t, :])), w_grouped[:, g, t])
                 quantise_chunk(w_grouped[:, g, t], w_codes[:, g, t], w_scales[:, g, t])
 
-        def multiply(g, t0):
-            for t in (t0, t0 + 1):
+        def multiply(g, u):
+            for e in range(2):
                 for c in range(PASSES):
                     nc.tensor.matmul_mx(
-                        out=h_ps[g][:, t, :],
-                        lhsT=w_codes[:, g, t, c, :].bitcast(FP8X4),
-                        lhsT_scale=w_scales[:, g, t, c, :],
+                        out=h_ps[2 * g + u][:, e, :],
+                        lhsT=w_codes[:, g, 2 * u + e, c, :].bitcast(FP8X4),
+                        lhsT_scale=w_scales[:, g, 2 * u + e, c, :],
                         rhs=x_codes[:, c, :].bitcast(FP8X4),
                         rhs_scale=x_scales[:, c, :],
                         start=(c == 0),
                         stop=(c == PASSES - 1),
                     )
 
-        prepare(0, 0)
-        prepare(0, 2)
-        multiply(0, 0)
-        mid = build_mid()
-        prepare(1, 0)
-        multiply(0, 2)
-        prepare(1, 2)
-        multiply(1, 0)
-        multiply(1, 2)
+        rot = keep.tile([P, ROT9 + 1, 3], F32)
 
-        wo_banks = [transpose_chunk(alternate_blocks(wo_sb[:, c, :])) for c in range(PACK)]
+        def build_rot():
+            rot_ps = ring.tile([P, ROT9 + 1, 2], F32, name="bank")
+            for g in range(HALVES):
+                for u in range(2):
+                    first = (TABLE // 2) * g + u
+                    rows_to_columns(rot_ps[:, 2 * g + u, :], tab[:, 0, first : first + 2 * P - 1 : 2], 0)
+                rows_to_columns(rot_ps[:, ROT1 + g, :], tab[:, 0, g * P : (g + 1) * P], 1)
+            rows_to_columns(rot_ps[:, ROT9, :], tab[:, 0, 0:1].to_broadcast([P, P]), LAST)
+            nc.vector.tensor_copy(out=rot[:, :, COS : NEG_SIN + 1], in_=rot_ps[:])
+            nc.vector.tensor_scalar_mul(out=rot[:, :, SIN], in0=rot[:, :, NEG_SIN], scalar1=-1.0)
 
-        def rotate(dst, src, cos_src, first, second, which):
-            for mine, partner, sine in ((second, first, NEG_SIN), (first, second, SIN)):
-                nc.vector.scalar_tensor_tensor(
-                    out=dst[:, mine, :],
-                    in0=src[:, partner, :],
-                    scalar=rot[:, which, sine : sine + 1],
-                    in1=cos_src[:, mine, :],
-                    op0=MULT,
-                    op1=ADD,
-                )
+        def factors_to_columns():
+            factor_ps = ring.tile([P, HALVES, MID, 2], F32, name="bank")
+            for m in range(MID):
+                for g in range(HALVES):
+                    rows_to_columns(factor_ps[:, g, m, :], spread[:, m, g * P : (g + 1) * P], FIRST_MID + m)
+            return factor_ps
+
+        def outer(groups, high, low, tables):
+            wider = keep.tile([P, groups, high, low], F32, name="outer%d" % low)
+            two = tables.rearrange("p (k two) w -> p k two w", two=2)
+            nc.vector.tensor_tensor(
+                out=wider[:],
+                in0=two[:, :, 1, 0:high].unsqueeze(3).to_broadcast([P, groups, high, low]),
+                in1=two[:, :, 0, :].unsqueeze(2).to_broadcast([P, groups, high, low]),
+                op=MULT,
+            )
+            return wider[:].rearrange("p k a b -> p k (a b)")
+
+        def build_mid(factor_ps):
+            nc.vector.tensor_copy(out=factor[:, :, 0:MID, :], in_=factor_ps[:])
+            bits2 = outer(4 * HALVES, 2, 2, factor[:].rearrange("p g m e -> p (g m) e"))
+            bits4 = outer(2 * HALVES, 4, 4, bits2)
+            return outer(HALVES, 8, 16, bits4)
+
+        def scale_by_cos(dst, src, which):
+            nc.scalar.activation(out=dst, in_=src, func=COPY, scale=rot[:, which, COS : COS + 1])
+
+        def add_partner(dst, partner, sine, which, scaled):
+            nc.vector.scalar_tensor_tensor(
+                out=dst, in0=partner, scalar=rot[:, which, sine : sine + 1], in1=scaled, op0=MULT, op1=ADD
+            )
 
         cos_h = keep.tile([P, HALVES, PACK, BATCH], F32)
         after0 = keep.tile([P, HALVES, PACK, BATCH], F32)
         cos_0 = keep.tile([P, HALVES, PACK, BATCH], F32)
         after1 = keep.tile([P, HALVES, PACK, BATCH], F32)
-        for g in range(HALVES):
-            for u in range(2):
-                nc.scalar.activation(
-                    out=cos_h[:, g, 2 * u : 2 * u + 2, :],
-                    in_=h_ps[g][:, 2 * u : 2 * u + 2, :],
-                    func=COPY,
-                    scale=rot[:, 2 * g + u, COS : COS + 1],
-                )
-            for u in (1, 0):
-                rotate(after0[:, g], h_ps[g], cos_h[:, g], 2 * u, 2 * u + 1, 2 * g + u)
-        for g in range(HALVES):
-            nc.scalar.activation(
-                out=cos_0[:, g], in_=after0[:, g], func=COPY, scale=rot[:, ROT1 + g, COS : COS + 1]
-            )
-            rotate(after1[:, g], after0[:, g], cos_0[:, g], slice(0, 2), slice(2, 4), ROT1 + g)
+        LOW, HIGH = slice(0, 2), slice(2, 4)
 
-        z_ps = [fixed.tile([P, PACK, BATCH], F32, name="z%d" % g, tag="z%d" % g) for g in range(HALVES)]
-        for g in range(HALVES):
-            nc.tensor.matmul(
-                out=z_ps[g][:].rearrange("p t n -> p (t n)"),
-                lhsT=mid[:, g, :],
-                rhs=after1[:, g].rearrange("p t n -> p (t n)"),
-                start=True,
-                stop=True,
-            )
+        def stage0(g, u):
+            which = 2 * g + u
+            h = h_ps[which]
+            scale_by_cos(cos_h[:, g, 2 * u : 2 * u + 2, :], h[:], which)
+            add_partner(after0[:, g, 2 * u, :], h[:, 1, :], SIN, which, cos_h[:, g, 2 * u, :])
+            add_partner(after0[:, g, 2 * u + 1, :], h[:, 0, :], NEG_SIN, which, cos_h[:, g, 2 * u + 1, :])
+
+        def stage1(g):
+            which = ROT1 + g
+            scale_by_cos(cos_0[:, g, LOW, :], after0[:, g, LOW, :], which)
+            scale_by_cos(cos_0[:, g, HIGH, :], after0[:, g, HIGH, :], which)
+            add_partner(after1[:, g, LOW, :], after0[:, g, HIGH, :], SIN, which, cos_0[:, g, LOW, :])
+            add_partner(after1[:, g, HIGH, :], after0[:, g, LOW, :], NEG_SIN, which, cos_0[:, g, HIGH, :])
+
+        z_ps = []
+
+        def stages2to8(g):
+            z = fixed.tile([P, PACK, BATCH], F32, name="z%d" % g, tag="piece%d" % g)
+            for quarters in (LOW, HIGH):
+                nc.tensor.matmul(
+                    out=z[:, quarters, :].rearrange("p t n -> p (t n)"),
+                    lhsT=mid[:, g, :],
+                    rhs=after1[:, g, quarters, :].rearrange("p t n -> p (t n)"),
+                    start=True,
+                    stop=True,
+                )
+            z_ps.append(z)
+
+        regroup_chunk(transpose_chunk(neighbouring_blocks(x_sb[:])), x_grouped[:])
+        quantise_chunk(x_grouped[:], x_codes[:], x_scales[:])
+        prepare(0, 0)
+        build_rot()
+        prepare(0, 1)
+        multiply(0, 0)
+        stage0(0, 0)
+        prepare(1, 0)
+        multiply(0, 1)
+        stage0(0, 1)
+        prepare(1, 1)
+        factor_ps = factors_to_columns()
+        multiply(1, 0)
+        mid = build_mid(factor_ps)
+        stage1(0)
+        stage0(1, 0)
+        multiply(1, 1)
+        wo_banks = [transpose_chunk(alternate_blocks(wo_sb[:, c, :])) for c in range(PACK)]
+        stages2to8(0)
+        stage0(1, 1)
+        stage1(1)
+        stages2to8(1)
 
         wo_grouped = keep.tile([P, PACK, PASSES, P, PACK], BF16, align_bytes=64)
         wo_codes = keep.tile([P, PACK, PASSES, P], U32, align_bytes=64)
@@ -257,14 +272,7 @@ def tile_butterflylayer_s_kernel(tc, x, w_in, w_out, b_out, a_pad, b_pad, out):
             nc.scalar.activation(
                 out=from_z0[:, g], in_=z0, func=COPY, scale=rot[:, ROT9, of_z0 : of_z0 + 1]
             )
-            nc.vector.scalar_tensor_tensor(
-                out=h_grouped[:, g],
-                in0=z1,
-                scalar=rot[:, ROT9, of_z1 : of_z1 + 1],
-                in1=from_z0[:, g],
-                op0=MULT,
-                op1=ADD,
-            )
+            add_partner(h_grouped[:, g], z1, of_z1, ROT9, from_z0[:, g])
         for g in range(HALVES):
             nc.vector.quantize_mx(
                 out=h_codes[:, g, :].bitcast(FP8X4),
@@ -275,7 +283,7 @@ def tile_butterflylayer_s_kernel(tc, x, w_in, w_out, b_out, a_pad, b_pad, out):
             regroup_chunk(wo_banks[c], wo_grouped[:, c])
             quantise_chunk(wo_grouped[:, c], wo_codes[:, c], wo_scales[:, c])
 
-        out_ps = [fixed.tile([P, 2, P], F32, name="out_ps%d" % b, tag="h%d" % b) for b in range(2)]
+        out_ps = [fixed.tile([P, 2, P], F32, name="out_ps%d" % b, tag="piece%d" % (2 + b)) for b in range(2)]
         out_sb = keep.tile([P, N_OUT], F32)
         for c in range(PACK):
             for g in range(HALVES):

@@ -52,17 +52,16 @@ def tile_butterflylayer_s_kernel(tc, x, w_in, w_out, b_out, a_pad, b_pad, out):
 
         x_sb = keep.tile([P, K_IN], BF16)
         nc.sync.dma_start(out=x_sb[:], in_=x)
-        stages = a_pad.shape[0]
-        nc.scalar.dma_start(out=tab[0:stages, 0, :], in_=a_pad)
-        nc.scalar.dma_start(out=tab[0:stages, 1, :], in_=b_pad)
-        nc.scalar.dma_start(out=tab[MIRROR : MIRROR + stages, 0, :], in_=b_pad)
-        nc.scalar.dma_start(out=tab[MIRROR : MIRROR + stages, 1, :], in_=a_pad)
+        for row, first_half, second_half in ((0, a_pad, b_pad), (MIRROR, b_pad, a_pad)):
+            late = slice(row + FIRST_MID, row + LAST + 1)
+            nc.sync.dma_start(out=tab[late, 0, 0:P], in_=first_half[FIRST_MID : LAST + 1, 0:P])
+            nc.sync.dma_start(out=tab[late, 1, 0:P], in_=second_half[FIRST_MID : LAST + 1, 0:P])
+            nc.sync.dma_start(out=tab[row : row + FIRST_MID, 0, :], in_=first_half[0:FIRST_MID, :])
 
         w_sb = keep.tile([P, HALVES, PACK, K_IN], BF16)
         w_rows = w_in.rearrange("(g p t) k -> p g t k", g=HALVES, t=PACK)
-        for g in range(HALVES):
-            for t in range(0, PACK, 2):
-                nc.sync.dma_start(out=w_sb[:, g, t : t + 2, :], in_=w_rows[:, g, t : t + 2, :])
+        for g, quarters in ((0, slice(0, 2)), (0, slice(2, 4)), (1, slice(0, 2)), (1, slice(2, 3)), (1, slice(3, 4))):
+            nc.sync.dma_start(out=w_sb[:, g, quarters, :], in_=w_rows[:, g, quarters, :])
         wo_sb = keep.tile([P, PACK, FEAT], BF16)
         wo_rows = w_out.rearrange("(c r) k -> r c k", c=PACK)
         for c in range(0, PACK, 2):
@@ -176,7 +175,7 @@ def tile_butterflylayer_s_kernel(tc, x, w_in, w_out, b_out, a_pad, b_pad, out):
         def outer(groups, high, low, tables):
             wider = keep.tile([P, groups, high, low], F32, name="outer%d" % low)
             two = tables.rearrange("p (k two) w -> p k two w", two=2)
-            nc.vector.tensor_tensor(
+            nc.gpsimd.tensor_tensor(
                 out=wider[:],
                 in0=two[:, :, 1, 0:high].unsqueeze(3).to_broadcast([P, groups, high, low]),
                 in1=two[:, :, 0, :].unsqueeze(2).to_broadcast([P, groups, high, low]),
@@ -202,7 +201,7 @@ def tile_butterflylayer_s_kernel(tc, x, w_in, w_out, b_out, a_pad, b_pad, out):
         after0 = keep.tile([P, HALVES, PACK, BATCH], F32)
         cos_0 = keep.tile([P, HALVES, PACK, BATCH], F32)
         after1 = keep.tile([P, HALVES, PACK, BATCH], F32)
-        LOW, HIGH = slice(0, 2), slice(2, 4)
+        LOW, HIGH, ALL = slice(0, 2), slice(2, 4), slice(0, 4)
 
         def stage0(g, u):
             which = 2 * g + u
@@ -211,10 +210,10 @@ def tile_butterflylayer_s_kernel(tc, x, w_in, w_out, b_out, a_pad, b_pad, out):
             add_partner(after0[:, g, 2 * u, :], h[:, 1, :], SIN, which, cos_h[:, g, 2 * u, :])
             add_partner(after0[:, g, 2 * u + 1, :], h[:, 0, :], NEG_SIN, which, cos_h[:, g, 2 * u + 1, :])
 
-        def stage1(g):
+        def stage1(g, scalar_pieces):
             which = ROT1 + g
-            scale_by_cos(cos_0[:, g, LOW, :], after0[:, g, LOW, :], which)
-            scale_by_cos(cos_0[:, g, HIGH, :], after0[:, g, HIGH, :], which)
+            for quarters in scalar_pieces:
+                scale_by_cos(cos_0[:, g, quarters, :], after0[:, g, quarters, :], which)
             add_partner(after1[:, g, LOW, :], after0[:, g, HIGH, :], SIN, which, cos_0[:, g, LOW, :])
             add_partner(after1[:, g, HIGH, :], after0[:, g, LOW, :], NEG_SIN, which, cos_0[:, g, HIGH, :])
 
@@ -243,17 +242,17 @@ def tile_butterflylayer_s_kernel(tc, x, w_in, w_out, b_out, a_pad, b_pad, out):
         multiply(0, 1)
         stage0(0, 1)
         prepare(1, 1)
-        factor_ps = factors_to_columns()
         multiply(1, 0)
-        mid = build_mid(factor_ps)
-        stage1(0)
+        mid = build_mid(factors_to_columns())
         stage0(1, 0)
+        stage1(0, (ALL,))
         multiply(1, 1)
-        wo_banks = [transpose_chunk(alternate_blocks(wo_sb[:, c, :])) for c in range(PACK)]
+        wo_banks = [transpose_chunk(alternate_blocks(wo_sb[:, c, :])) for c in (0, 1)]
         stages2to8(0)
         stage0(1, 1)
-        stage1(1)
+        stage1(1, (LOW, HIGH))
         stages2to8(1)
+        wo_banks.extend([transpose_chunk(alternate_blocks(wo_sb[:, c, :])) for c in (2, 3)])
 
         wo_grouped = keep.tile([P, PACK, PASSES, P, PACK], BF16, align_bytes=64)
         wo_codes = keep.tile([P, PACK, PASSES, P], U32, align_bytes=64)

@@ -236,12 +236,12 @@ def tile_butterflylayer_s_kernel(tc, x, w_in, w_out, b_out, a_pad, b_pad, out):
         prepare(0, 0)
         build_rot()
         prepare(0, 1)
+        prepare(1, 0)
         multiply(0, 0)
         stage0(0, 0)
-        prepare(1, 0)
+        prepare(1, 1)
         multiply(0, 1)
         stage0(0, 1)
-        prepare(1, 1)
         multiply(1, 0)
         mid = build_mid(factors_to_columns())
         stage0(1, 0)

@@ -114,14 +114,12 @@ def tile_butterflylayer_s_kernel(tc, x, w_in, w_out, b_out, a_pad, b_pad, out):
             entries = P >> m
             repeat = 1 << m
             src = tab[:, :, 0:entries].rearrange("p e v -> p v e").unsqueeze(3)
-            nc.gpsimd.tensor_scalar(
-                out=spread[:, m, :].rearrange("p (v e w) -> p v e w", e=2, w=repeat),
-                in0=src.to_broadcast([P, entries, 2, repeat]),
-                scalar1=1.0,
-                scalar2=0.0,
-                op0=MULT,
-                op1=ADD,
-            )
+            src = src.to_broadcast([P, entries, 2, repeat])
+            dst = spread[:, m, :].rearrange("p (v e w) -> p v e w", e=2, w=repeat)
+            if m % 2 == 0:
+                nc.gpsimd.tensor_scalar(out=dst, in0=src, scalar1=1.0, scalar2=0.0, op0=MULT, op1=ADD)
+            else:
+                nc.vector.tensor_copy(out=dst, in_=src)
 
         x_grouped = keep.tile([P, PASSES, BATCH, PACK], BF16, align_bytes=64)
         x_codes = keep.tile([P, PASSES, BATCH], U32, align_bytes=64)
@@ -165,15 +163,8 @@ def tile_butterflylayer_s_kernel(tc, x, w_in, w_out, b_out, a_pad, b_pad, out):
             nc.vector.tensor_copy(out=rot[:, :, COS : NEG_SIN + 1], in_=rot_ps[:])
             nc.vector.tensor_scalar_mul(out=rot[:, :, SIN], in0=rot[:, :, NEG_SIN], scalar1=-1.0)
 
-        def factors_to_columns():
-            factor_ps = ring.tile([P, HALVES, MID, 2], F32, name="bank")
-            for m in range(MID):
-                for g in range(HALVES):
-                    rows_to_columns(factor_ps[:, g, m, :], spread[:, m, g * P : (g + 1) * P], FIRST_MID + m)
-            return factor_ps
-
-        def outer(groups, high, low, tables):
-            wider = keep.tile([P, groups, high, low], F32, name="outer%d" % low)
+        def outer(g, groups, high, low, tables):
+            wider = keep.tile([P, groups, high, low], F32, name="outer%d_%d" % (low, g))
             two = tables.rearrange("p (k two) w -> p k two w", two=2)
             nc.gpsimd.tensor_tensor(
                 out=wider[:],
@@ -183,11 +174,14 @@ def tile_butterflylayer_s_kernel(tc, x, w_in, w_out, b_out, a_pad, b_pad, out):
             )
             return wider[:].rearrange("p k a b -> p k (a b)")
 
-        def build_mid(factor_ps):
-            nc.vector.tensor_copy(out=factor[:, :, 0:MID, :], in_=factor_ps[:])
-            bits2 = outer(4 * HALVES, 2, 2, factor[:].rearrange("p g m e -> p (g m) e"))
-            bits4 = outer(2 * HALVES, 4, 4, bits2)
-            return outer(HALVES, 8, 16, bits4)
+        def build_mid(g):
+            factor_ps = ring.tile([P, MID, 2], F32, name="bank")
+            for m in range(MID):
+                rows_to_columns(factor_ps[:, m, :], spread[:, m, g * P : (g + 1) * P], FIRST_MID + m)
+            nc.vector.tensor_copy(out=factor[:, g, 0:MID, :], in_=factor_ps[:])
+            bits2 = outer(g, 4, 2, 2, factor[:, g])
+            bits4 = outer(g, 2, 4, 4, bits2)
+            return outer(g, 1, 8, 16, bits4)[:, 0, :]
 
         def scale_by_cos(dst, src, which):
             nc.scalar.activation(out=dst, in_=src, func=COPY, scale=rot[:, which, COS : COS + 1])
@@ -199,9 +193,9 @@ def tile_butterflylayer_s_kernel(tc, x, w_in, w_out, b_out, a_pad, b_pad, out):
 
         cos_h = keep.tile([P, HALVES, PACK, BATCH], F32)
         after0 = keep.tile([P, HALVES, PACK, BATCH], F32)
-        cos_0 = keep.tile([P, HALVES, PACK, BATCH], F32)
+        share1 = keep.tile([P, HALVES, 2, 2, BATCH], F32)
         after1 = keep.tile([P, HALVES, PACK, BATCH], F32)
-        LOW, HIGH, ALL = slice(0, 2), slice(2, 4), slice(0, 4)
+        LOW, HIGH = slice(0, 2), slice(2, 4)
 
         def stage0(g, u):
             which = 2 * g + u
@@ -210,12 +204,15 @@ def tile_butterflylayer_s_kernel(tc, x, w_in, w_out, b_out, a_pad, b_pad, out):
             add_partner(after0[:, g, 2 * u, :], h[:, 1, :], SIN, which, cos_h[:, g, 2 * u, :])
             add_partner(after0[:, g, 2 * u + 1, :], h[:, 0, :], NEG_SIN, which, cos_h[:, g, 2 * u + 1, :])
 
-        def stage1(g, scalar_pieces):
-            which = ROT1 + g
-            for quarters in scalar_pieces:
-                scale_by_cos(cos_0[:, g, quarters, :], after0[:, g, quarters, :], which)
-            add_partner(after1[:, g, LOW, :], after0[:, g, HIGH, :], SIN, which, cos_0[:, g, LOW, :])
-            add_partner(after1[:, g, HIGH, :], after0[:, g, LOW, :], NEG_SIN, which, cos_0[:, g, HIGH, :])
+        def stage1_early(g):
+            for k, column in ((0, COS), (1, NEG_SIN)):
+                nc.vector.tensor_scalar_mul(
+                    out=share1[:, g, k], in0=after0[:, g, LOW, :], scalar1=rot[:, ROT1 + g, column : column + 1]
+                )
+
+        def stage1_late(g):
+            add_partner(after1[:, g, LOW, :], after0[:, g, HIGH, :], SIN, ROT1 + g, share1[:, g, 0])
+            add_partner(after1[:, g, HIGH, :], after0[:, g, HIGH, :], COS, ROT1 + g, share1[:, g, 1])
 
         z_ps = []
 
@@ -224,7 +221,7 @@ def tile_butterflylayer_s_kernel(tc, x, w_in, w_out, b_out, a_pad, b_pad, out):
             for quarters in (LOW, HIGH):
                 nc.tensor.matmul(
                     out=z[:, quarters, :].rearrange("p t n -> p (t n)"),
-                    lhsT=mid[:, g, :],
+                    lhsT=mid[g],
                     rhs=after1[:, g, quarters, :].rearrange("p t n -> p (t n)"),
                     start=True,
                     stop=True,
@@ -233,24 +230,28 @@ def tile_butterflylayer_s_kernel(tc, x, w_in, w_out, b_out, a_pad, b_pad, out):
 
         regroup_chunk(transpose_chunk(neighbouring_blocks(x_sb[:])), x_grouped[:])
         quantise_chunk(x_grouped[:], x_codes[:], x_scales[:])
+        mid = []
         prepare(0, 0)
         build_rot()
         prepare(0, 1)
-        prepare(1, 0)
+        mid.append(build_mid(0))
         multiply(0, 0)
         stage0(0, 0)
-        prepare(1, 1)
+        stage1_early(0)
+        prepare(1, 0)
         multiply(0, 1)
         stage0(0, 1)
+        prepare(1, 1)
+        mid.append(build_mid(1))
+        stage1_late(0)
         multiply(1, 0)
-        mid = build_mid(factors_to_columns())
         stage0(1, 0)
-        stage1(0, (ALL,))
+        stage1_early(1)
         multiply(1, 1)
         wo_banks = [transpose_chunk(alternate_blocks(wo_sb[:, c, :])) for c in (0, 1)]
         stages2to8(0)
         stage0(1, 1)
-        stage1(1, (LOW, HIGH))
+        stage1_late(1)
         stages2to8(1)
         wo_banks.extend([transpose_chunk(alternate_blocks(wo_sb[:, c, :])) for c in (2, 3)])
 

@@ -22,14 +22,13 @@ FEAT = 1024
 N_OUT = 512
 PASSES = K_IN // K_PASS
 HALVES = FEAT // K_PASS
-TABLE = 512
 MID = 7
 FIRST_MID = 2
 LAST = 9
-MIRROR = 32
+TAIL = LAST - FIRST_MID + 1
+HALF_ROW = 64
 COS, NEG_SIN, SIN = 0, 1, 2
-ROT1 = 4
-ROT9 = 6
+ROT1, ROT9, ROT_END = 12, 18, 21
 
 FLOPS = 2 * BATCH * K_IN * FEAT + 2 * BATCH * FEAT * N_OUT + 6 * BATCH * (FEAT // 2) * 10
 
@@ -42,26 +41,28 @@ def tile_butterflylayer_s_kernel(tc, x, w_in, w_out, b_out, a_pad, b_pad, out):
         fixed = ctx.enter_context(tc.psum_pool(name="fixed", bufs=1))
         ctx.enter_context(tc.manual_schedule())
 
-        tab = keep.tile([P, 2, TABLE], BF16)
+        tab = keep.tile([P, 2, 3, HALF_ROW], BF16)
         nc.vector.memset(tab[:].bitcast(I32), 0)
-        sign = keep.tile([P, 1], F32)
-        nc.vector.memset(sign[:], 1.0)
-        nc.vector.memset(sign[MIRROR : 2 * MIRROR, :], -1.0)
-        factor = keep.tile([P, HALVES, MID + 1, 2], F32)
-        nc.vector.memset(factor[:], 1.0)
+        early = keep.tile([P, 2 * P], BF16)
+        nc.vector.memset(early[:].bitcast(I32), 0)
 
         x_sb = keep.tile([P, K_IN], BF16)
         nc.sync.dma_start(out=x_sb[:], in_=x)
-        for row, first_half, second_half in ((0, a_pad, b_pad), (MIRROR, b_pad, a_pad)):
-            late = slice(row + FIRST_MID, row + LAST + 1)
-            nc.sync.dma_start(out=tab[late, 0, 0:P], in_=first_half[FIRST_MID : LAST + 1, 0:P])
-            nc.sync.dma_start(out=tab[late, 1, 0:P], in_=second_half[FIRST_MID : LAST + 1, 0:P])
-            nc.sync.dma_start(out=tab[row : row + FIRST_MID, 0, :], in_=first_half[0:FIRST_MID, :])
-
         w_sb = keep.tile([P, HALVES, PACK, K_IN], BF16)
         w_rows = w_in.rearrange("(g p t) k -> p g t k", g=HALVES, t=PACK)
         for g, quarters in ((0, slice(0, 2)), (0, slice(2, 4)), (1, slice(0, 2)), (1, slice(2, 3)), (1, slice(3, 4))):
             nc.sync.dma_start(out=w_sb[:, g, quarters, :], in_=w_rows[:, g, quarters, :])
+            if g == 0 and quarters.start == 0:
+                for piece, pad in ((0, a_pad), (1, b_pad), (2, a_pad)):
+                    nc.sync.dma_start(
+                        out=tab[0:TAIL, :, piece, :],
+                        in_=pad[FIRST_MID : LAST + 1, 0:P].rearrange("l (h v) -> l h v", h=2),
+                    )
+                for row, pad in ((0, a_pad), (4, b_pad)):
+                    nc.sync.dma_start(
+                        out=early[row : row + 4, :],
+                        in_=pad[0:FIRST_MID, :].rearrange("l (g c) -> (l g) c", g=2),
+                    )
         wo_sb = keep.tile([P, PACK, FEAT], BF16)
         wo_rows = w_out.rearrange("(c r) k -> r c k", c=PACK)
         for c in range(0, PACK, 2):
@@ -71,6 +72,13 @@ def tile_butterflylayer_s_kernel(tc, x, w_in, w_out, b_out, a_pad, b_pad, out):
 
         ident = keep.tile([P, P], F32)
         make_identity(nc, ident[:])
+        ident_bf = keep.tile([P, P], BF16)
+        nc.vector.tensor_copy(out=ident_bf[:], in_=ident[:])
+        sign = keep.tile([P, 2, 2, TAIL], F32)
+        nc.vector.memset(sign[:], 1.0)
+        nc.vector.memset(sign[0:HALF_ROW, :, 1, :], -1.0)
+        factor = keep.tile([P, HALVES, MID + 1, 2], F32)
+        nc.vector.memset(factor[:], 1.0)
 
         def neighbouring_blocks(rows):
             words = rows.bitcast(F32)
@@ -101,22 +109,19 @@ def tile_butterflylayer_s_kernel(tc, x, w_in, w_out, b_out, a_pad, b_pad, out):
                 in_=grouped.rearrange("p c r j -> p (c r j)"),
             )
 
-        pick = keep.tile([P, MIRROR, 2], BF16)
-        nc.vector.tensor_copy(out=pick[:], in_=ident[:, 0 : 2 * MIRROR].rearrange("p (e l) -> p l e", e=2))
-
-        def rows_to_columns(dst, src, level):
-            nc.tensor.matmul(out=dst, lhsT=src, rhs=pick[:, level, :], start=True, stop=True)
-
-        nc.vector.tensor_scalar_mul(out=tab[:, 0, :], in0=tab[:, 0, :], scalar1=sign[:, 0:1])
+        pick = keep.tile([P, 3, 4], BF16)
+        nc.vector.tensor_copy(out=pick[:, COS, :], in_=ident[:, 0:4])
+        nc.vector.tensor_scalar_mul(out=pick[:, NEG_SIN, :], in0=ident[:, 4:8], scalar1=-1.0)
+        nc.vector.tensor_copy(out=pick[:, SIN, :], in_=ident[:, 4:8])
 
         spread = keep.tile([P, MID, HALVES * P], BF16)
-        for m in range(MID):
-            entries = P >> m
+        for m in (0, 1, 2, 3, 4, 5, 6):
+            entries = min(P >> m, HALF_ROW)
             repeat = 1 << m
-            src = tab[:, :, 0:entries].rearrange("p e v -> p v e").unsqueeze(3)
+            src = ident_bf[:].rearrange("p (e v) -> p v e", e=2)[:, 0:entries, :].unsqueeze(3)
             src = src.to_broadcast([P, entries, 2, repeat])
-            dst = spread[:, m, :].rearrange("p (v e w) -> p v e w", e=2, w=repeat)
-            if m % 2 == 0:
+            dst = spread[:, m, 0 : entries * 2 * repeat].rearrange("p (v e w) -> p v e w", e=2, w=repeat)
+            if m in (2, 4, 6):
                 nc.gpsimd.tensor_scalar(out=dst, in0=src, scalar1=1.0, scalar2=0.0, op0=MULT, op1=ADD)
             else:
                 nc.vector.tensor_copy(out=dst, in_=src)
@@ -132,10 +137,17 @@ def tile_butterflylayer_s_kernel(tc, x, w_in, w_out, b_out, a_pad, b_pad, out):
             for piece in range(2 * HALVES)
         ]
 
-        def prepare(g, u):
-            for t in (2 * u, 2 * u + 1):
-                regroup_chunk(transpose_chunk(neighbouring_blocks(w_sb[:, g, t, :])), w_grouped[:, g, t])
+        def transpose_piece(g, u):
+            return [transpose_chunk(neighbouring_blocks(w_sb[:, g, t, :])) for t in (2 * u, 2 * u + 1)]
+
+        def quantise_piece(g, u, banks):
+            for e in range(2):
+                t = 2 * u + e
+                regroup_chunk(banks[e], w_grouped[:, g, t])
                 quantise_chunk(w_grouped[:, g, t], w_codes[:, g, t], w_scales[:, g, t])
+
+        def prepare(g, u):
+            quantise_piece(g, u, transpose_piece(g, u))
 
         def multiply(g, u):
             for e in range(2):
@@ -150,21 +162,48 @@ def tile_butterflylayer_s_kernel(tc, x, w_in, w_out, b_out, a_pad, b_pad, out):
                         stop=(c == PASSES - 1),
                     )
 
-        rot = keep.tile([P, ROT9 + 1, 3], F32)
+        rot = keep.tile([P, ROT_END], F32)
+        columns = keep.tile([P, 2, 2, TAIL], BF16)
+
+        def build_columns():
+            col_ps = ring.tile([P, 2, 2, TAIL], F32, name="bank")
+            for h in range(2):
+                for o in range(2):
+                    nc.tensor.matmul(
+                        out=col_ps[:, h, o, :],
+                        lhsT=tab[:, h, o : o + 2, :].rearrange("p s v -> p (s v)"),
+                        rhs=ident_bf[:, 0:TAIL],
+                        start=True,
+                        stop=True,
+                    )
+            nc.vector.tensor_tensor(out=columns[:], in0=col_ps[:], in1=sign[:], op=MULT)
 
         def build_rot():
-            rot_ps = ring.tile([P, ROT9 + 1, 2], F32, name="bank")
+            rot_ps = ring.tile([P, ROT_END], F32, name="bank")
+            for u in range(2):
+                nc.tensor.matmul(
+                    out=rot_ps[:, 6 * u : 6 * u + 6], lhsT=early[:, u::2], rhs=pick[:, :, 0:2], start=True, stop=True
+                )
             for g in range(HALVES):
-                for u in range(2):
-                    first = (TABLE // 2) * g + u
-                    rows_to_columns(rot_ps[:, 2 * g + u, :], tab[:, 0, first : first + 2 * P - 1 : 2], 0)
-                rows_to_columns(rot_ps[:, ROT1 + g, :], tab[:, 0, g * P : (g + 1) * P], 1)
-            rows_to_columns(rot_ps[:, ROT9, :], tab[:, 0, 0:1].to_broadcast([P, P]), LAST)
-            nc.vector.tensor_copy(out=rot[:, :, COS : NEG_SIN + 1], in_=rot_ps[:])
-            nc.vector.tensor_scalar_mul(out=rot[:, :, SIN], in0=rot[:, :, NEG_SIN], scalar1=-1.0)
+                nc.tensor.matmul(
+                    out=rot_ps[:, ROT1 + 3 * g : ROT1 + 3 * g + 3],
+                    lhsT=early[:, g * P : (g + 1) * P],
+                    rhs=pick[:, :, 2],
+                    start=True,
+                    stop=True,
+                )
+            for row, first, count in ((0, COS, 2), (HALF_ROW, SIN, 1)):
+                nc.tensor.matmul(
+                    out=rot_ps[:, ROT9 + first : ROT9 + first + count],
+                    lhsT=ident_bf[:, row : row + 1].to_broadcast([P, P]),
+                    rhs=columns[:, 0, 0:count, TAIL - 1],
+                    start=True,
+                    stop=True,
+                )
+            nc.vector.tensor_copy(out=rot[:], in_=rot_ps[:])
 
-        def outer(g, groups, high, low, tables):
-            wider = keep.tile([P, groups, high, low], F32, name="outer%d_%d" % (low, g))
+        def outer(groups, high, low, tables):
+            wider = keep.tile([P, groups, high, low], F32, name="outer%d" % low)
             two = tables.rearrange("p (k two) w -> p k two w", two=2)
             nc.gpsimd.tensor_tensor(
                 out=wider[:],
@@ -174,22 +213,34 @@ def tile_butterflylayer_s_kernel(tc, x, w_in, w_out, b_out, a_pad, b_pad, out):
             )
             return wider[:].rearrange("p k a b -> p k (a b)")
 
-        def build_mid(g):
-            factor_ps = ring.tile([P, MID, 2], F32, name="bank")
-            for m in range(MID):
-                rows_to_columns(factor_ps[:, m, :], spread[:, m, g * P : (g + 1) * P], FIRST_MID + m)
-            nc.vector.tensor_copy(out=factor[:, g, 0:MID, :], in_=factor_ps[:])
-            bits2 = outer(g, 4, 2, 2, factor[:, g])
-            bits4 = outer(g, 2, 4, 4, bits2)
-            return outer(g, 1, 8, 16, bits4)[:, 0, :]
+        def build_mid():
+            factor_ps = ring.tile([P, HALVES, MID, 2], F32, name="bank")
+            for g in range(HALVES):
+                for m in range(MID):
+                    h, first = (g, 0) if m == 0 else (0, g * P)
+                    nc.tensor.matmul(
+                        out=factor_ps[:, g, m, :],
+                        lhsT=spread[:, m, first : first + P],
+                        rhs=columns[:, h, :, m],
+                        start=True,
+                        stop=True,
+                    )
+            nc.vector.tensor_copy(out=factor[:, :, 0:MID, :], in_=factor_ps[:])
+            bits2 = outer(HALVES * 4, 2, 2, factor[:].rearrange("p g m o -> p (g m) o"))
+            bits4 = outer(HALVES * 2, 4, 4, bits2)
+            return outer(HALVES, 8, 16, bits4)
 
-        def scale_by_cos(dst, src, which):
-            nc.scalar.activation(out=dst, in_=src, func=COPY, scale=rot[:, which, COS : COS + 1])
+        def rot0(g, u, kind):
+            return rot[:, 6 * u + 2 * kind + g : 6 * u + 2 * kind + g + 1]
 
-        def add_partner(dst, partner, sine, which, scaled):
-            nc.vector.scalar_tensor_tensor(
-                out=dst, in0=partner, scalar=rot[:, which, sine : sine + 1], in1=scaled, op0=MULT, op1=ADD
-            )
+        def rot1(g, kind):
+            return rot[:, ROT1 + 3 * g + kind : ROT1 + 3 * g + kind + 1]
+
+        def rot9(kind):
+            return rot[:, ROT9 + kind : ROT9 + kind + 1]
+
+        def add_partner(dst, partner, sine, scaled):
+            nc.vector.scalar_tensor_tensor(out=dst, in0=partner, scalar=sine, in1=scaled, op0=MULT, op1=ADD)
 
         cos_h = keep.tile([P, HALVES, PACK, BATCH], F32)
         after0 = keep.tile([P, HALVES, PACK, BATCH], F32)
@@ -198,21 +249,22 @@ def tile_butterflylayer_s_kernel(tc, x, w_in, w_out, b_out, a_pad, b_pad, out):
         LOW, HIGH = slice(0, 2), slice(2, 4)
 
         def stage0(g, u):
-            which = 2 * g + u
-            h = h_ps[which]
-            scale_by_cos(cos_h[:, g, 2 * u : 2 * u + 2, :], h[:], which)
-            add_partner(after0[:, g, 2 * u, :], h[:, 1, :], SIN, which, cos_h[:, g, 2 * u, :])
-            add_partner(after0[:, g, 2 * u + 1, :], h[:, 0, :], NEG_SIN, which, cos_h[:, g, 2 * u + 1, :])
+            h = h_ps[2 * g + u]
+            nc.scalar.activation(
+                out=cos_h[:, g, 2 * u : 2 * u + 2, :], in_=h[:], func=COPY, scale=rot0(g, u, COS)
+            )
+            add_partner(after0[:, g, 2 * u, :], h[:, 1, :], rot0(g, u, SIN), cos_h[:, g, 2 * u, :])
+            add_partner(after0[:, g, 2 * u + 1, :], h[:, 0, :], rot0(g, u, NEG_SIN), cos_h[:, g, 2 * u + 1, :])
 
         def stage1_early(g):
-            for k, column in ((0, COS), (1, NEG_SIN)):
+            for k, kind in ((0, COS), (1, NEG_SIN)):
                 nc.vector.tensor_scalar_mul(
-                    out=share1[:, g, k], in0=after0[:, g, LOW, :], scalar1=rot[:, ROT1 + g, column : column + 1]
+                    out=share1[:, g, k], in0=after0[:, g, LOW, :], scalar1=rot1(g, kind)
                 )
 
         def stage1_late(g):
-            add_partner(after1[:, g, LOW, :], after0[:, g, HIGH, :], SIN, ROT1 + g, share1[:, g, 0])
-            add_partner(after1[:, g, HIGH, :], after0[:, g, HIGH, :], COS, ROT1 + g, share1[:, g, 1])
+            add_partner(after1[:, g, LOW, :], after0[:, g, HIGH, :], rot1(g, SIN), share1[:, g, 0])
+            add_partner(after1[:, g, HIGH, :], after0[:, g, HIGH, :], rot1(g, COS), share1[:, g, 1])
 
         z_ps = []
 
@@ -221,7 +273,7 @@ def tile_butterflylayer_s_kernel(tc, x, w_in, w_out, b_out, a_pad, b_pad, out):
             for quarters in (LOW, HIGH):
                 nc.tensor.matmul(
                     out=z[:, quarters, :].rearrange("p t n -> p (t n)"),
-                    lhsT=mid[g],
+                    lhsT=mid[:, g, :],
                     rhs=after1[:, g, quarters, :].rearrange("p t n -> p (t n)"),
                     start=True,
                     stop=True,
@@ -230,11 +282,13 @@ def tile_butterflylayer_s_kernel(tc, x, w_in, w_out, b_out, a_pad, b_pad, out):
 
         regroup_chunk(transpose_chunk(neighbouring_blocks(x_sb[:])), x_grouped[:])
         quantise_chunk(x_grouped[:], x_codes[:], x_scales[:])
-        mid = []
-        prepare(0, 0)
+        banks = transpose_piece(0, 0)
+        build_columns()
+        quantise_piece(0, 0, banks)
         build_rot()
-        prepare(0, 1)
-        mid.append(build_mid(0))
+        banks = transpose_piece(0, 1)
+        mid = build_mid()
+        quantise_piece(0, 1, banks)
         multiply(0, 0)
         stage0(0, 0)
         stage1_early(0)
@@ -242,7 +296,6 @@ def tile_butterflylayer_s_kernel(tc, x, w_in, w_out, b_out, a_pad, b_pad, out):
         multiply(0, 1)
         stage0(0, 1)
         prepare(1, 1)
-        mid.append(build_mid(1))
         stage1_late(0)
         multiply(1, 0)
         stage0(1, 0)
@@ -270,9 +323,9 @@ def tile_butterflylayer_s_kernel(tc, x, w_in, w_out, b_out, a_pad, b_pad, out):
         h_scales = keep.tile([P, HALVES, BATCH], U8, align_bytes=64)
         for g, of_z0, of_z1 in ((0, COS, SIN), (1, NEG_SIN, COS)):
             nc.scalar.activation(
-                out=from_z0[:, g], in_=z0, func=COPY, scale=rot[:, ROT9, of_z0 : of_z0 + 1]
+                out=from_z0[:, g], in_=z0, func=COPY, scale=rot9(of_z0)
             )
-            add_partner(h_grouped[:, g], z1, of_z1, ROT9, from_z0[:, g])
+            add_partner(h_grouped[:, g], z1, rot9(of_z1), from_z0[:, g])
         for g in range(HALVES):
             nc.vector.quantize_mx(
                 out=h_codes[:, g, :].bitcast(FP8X4),

@@ -132,10 +132,7 @@ def tile_butterflylayer_s_kernel(tc, x, w_in, w_out, b_out, a_pad, b_pad, out):
         w_grouped = keep.tile([P, HALVES, PACK, PASSES, P, PACK], BF16, align_bytes=64)
         w_codes = keep.tile([P, HALVES, PACK, PASSES, P], U32, align_bytes=64)
         w_scales = keep.tile([P, HALVES, PACK, PASSES, P], U8, align_bytes=64)
-        h_ps = [
-            fixed.tile([P, 2, BATCH], F32, name="h%d" % piece, tag="piece%d" % piece)
-            for piece in range(2 * HALVES)
-        ]
+        h_ps = {}
 
         def transpose_piece(g, u):
             return [transpose_chunk(neighbouring_blocks(w_sb[:, g, t, :])) for t in (2 * u, 2 * u + 1)]
@@ -146,14 +143,12 @@ def tile_butterflylayer_s_kernel(tc, x, w_in, w_out, b_out, a_pad, b_pad, out):
                 regroup_chunk(banks[e], w_grouped[:, g, t])
                 quantise_chunk(w_grouped[:, g, t], w_codes[:, g, t], w_scales[:, g, t])
 
-        def prepare(g, u):
-            quantise_piece(g, u, transpose_piece(g, u))
-
         def multiply(g, u):
+            h_ps[g, u] = fixed.tile([P, 2, BATCH], F32, name="h%d%d" % (g, u), tag="piece%d" % (2 * g + u))
             for e in range(2):
                 for c in range(PASSES):
                     nc.tensor.matmul_mx(
-                        out=h_ps[2 * g + u][:, e, :],
+                        out=h_ps[g, u][:, e, :],
                         lhsT=w_codes[:, g, 2 * u + e, c, :].bitcast(FP8X4),
                         lhsT_scale=w_scales[:, g, 2 * u + e, c, :],
                         rhs=x_codes[:, c, :].bitcast(FP8X4),
@@ -166,7 +161,7 @@ def tile_butterflylayer_s_kernel(tc, x, w_in, w_out, b_out, a_pad, b_pad, out):
         columns = keep.tile([P, 2, 2, TAIL], BF16)
 
         def build_columns():
-            col_ps = ring.tile([P, 2, 2, TAIL], F32, name="bank")
+            col_ps = fixed.tile([P, 2, 2, TAIL], F32, name="col_ps", tag="piece1")
             for h in range(2):
                 for o in range(2):
                     nc.tensor.matmul(
@@ -179,7 +174,7 @@ def tile_butterflylayer_s_kernel(tc, x, w_in, w_out, b_out, a_pad, b_pad, out):
             nc.vector.tensor_tensor(out=columns[:], in0=col_ps[:], in1=sign[:], op=MULT)
 
         def build_rot():
-            rot_ps = ring.tile([P, ROT_END], F32, name="bank")
+            rot_ps = fixed.tile([P, ROT_END], F32, name="rot_ps", tag="piece2")
             for u in range(2):
                 nc.tensor.matmul(
                     out=rot_ps[:, 6 * u : 6 * u + 6], lhsT=early[:, u::2], rhs=pick[:, :, 0:2], start=True, stop=True
@@ -214,7 +209,7 @@ def tile_butterflylayer_s_kernel(tc, x, w_in, w_out, b_out, a_pad, b_pad, out):
             return wider[:].rearrange("p k a b -> p k (a b)")
 
         def build_mid():
-            factor_ps = ring.tile([P, HALVES, MID, 2], F32, name="bank")
+            factor_ps = fixed.tile([P, HALVES, MID, 2], F32, name="factor_ps", tag="piece3")
             for g in range(HALVES):
                 for m in range(MID):
                     h, first = (g, 0) if m == 0 else (0, g * P)
@@ -245,11 +240,11 @@ def tile_butterflylayer_s_kernel(tc, x, w_in, w_out, b_out, a_pad, b_pad, out):
         cos_h = keep.tile([P, HALVES, PACK, BATCH], F32)
         after0 = keep.tile([P, HALVES, PACK, BATCH], F32)
         share1 = keep.tile([P, HALVES, 2, 2, BATCH], F32)
-        after1 = keep.tile([P, HALVES, PACK, BATCH], F32)
+        after1 = keep.tile([P, HALVES, 2, PACK, BATCH // 2], F32)
         LOW, HIGH = slice(0, 2), slice(2, 4)
 
         def stage0(g, u):
-            h = h_ps[2 * g + u]
+            h = h_ps[g, u]
             nc.scalar.activation(
                 out=cos_h[:, g, 2 * u : 2 * u + 2, :], in_=h[:], func=COPY, scale=rot0(g, u, COS)
             )
@@ -262,51 +257,67 @@ def tile_butterflylayer_s_kernel(tc, x, w_in, w_out, b_out, a_pad, b_pad, out):
                     out=share1[:, g, k], in0=after0[:, g, LOW, :], scalar1=rot1(g, kind)
                 )
 
-        def stage1_late(g):
-            add_partner(after1[:, g, LOW, :], after0[:, g, HIGH, :], rot1(g, SIN), share1[:, g, 0])
-            add_partner(after1[:, g, HIGH, :], after0[:, g, HIGH, :], rot1(g, COS), share1[:, g, 1])
-
-        z_ps = []
-
-        def stages2to8(g):
-            z = fixed.tile([P, PACK, BATCH], F32, name="z%d" % g, tag="piece%d" % g)
-            for quarters in (LOW, HIGH):
-                nc.tensor.matmul(
-                    out=z[:, quarters, :].rearrange("p t n -> p (t n)"),
-                    lhsT=mid[:, g, :],
-                    rhs=after1[:, g, quarters, :].rearrange("p t n -> p (t n)"),
-                    start=True,
-                    stop=True,
+        def stage1_late(g, half):
+            batch = slice(half * (BATCH // 2), (half + 1) * (BATCH // 2))
+            for k, (quarters, kind) in enumerate(((LOW, SIN), (HIGH, COS))):
+                add_partner(
+                    after1[:, g, half, quarters, :],
+                    after0[:, g, HIGH, batch],
+                    rot1(g, kind),
+                    share1[:, g, k, :, batch],
                 )
-            z_ps.append(z)
 
-        regroup_chunk(transpose_chunk(neighbouring_blocks(x_sb[:])), x_grouped[:])
-        quantise_chunk(x_grouped[:], x_codes[:], x_scales[:])
-        banks = transpose_piece(0, 0)
+        z_ps = {}
+
+        def stages2to8(g, half):
+            z_ps[g, half] = fixed.tile(
+                [P, PACK, BATCH // 2], F32, name="z%d_%d" % (g, half), tag="piece%d" % (2 * g + half)
+            )
+            nc.tensor.matmul(
+                out=z_ps[g, half][:].rearrange("p t n -> p (t n)"),
+                lhsT=mid[:, g, :],
+                rhs=after1[:, g, half].rearrange("p t n -> p (t n)"),
+                start=True,
+                stop=True,
+            )
+
+        for warm_up in range(3):
+            transpose_chunk([ident[:]] * 4)
+        x_bank = transpose_chunk(neighbouring_blocks(x_sb[:]))
+        banks = {(0, 0): transpose_piece(0, 0)}
         build_columns()
-        quantise_piece(0, 0, banks)
+        regroup_chunk(x_bank, x_grouped[:])
+        quantise_chunk(x_grouped[:], x_codes[:], x_scales[:])
+        quantise_piece(0, 0, banks[0, 0])
+        banks[0, 1] = transpose_piece(0, 1)
         build_rot()
-        banks = transpose_piece(0, 1)
         mid = build_mid()
-        quantise_piece(0, 1, banks)
+        quantise_piece(0, 1, banks[0, 1])
         multiply(0, 0)
         stage0(0, 0)
         stage1_early(0)
-        prepare(1, 0)
+        banks[1, 0] = transpose_piece(1, 0)
+        quantise_piece(1, 0, banks[1, 0])
         multiply(0, 1)
         stage0(0, 1)
-        prepare(1, 1)
-        stage1_late(0)
+        banks[1, 1] = transpose_piece(1, 1)
+        quantise_piece(1, 1, banks[1, 1])
+        for half in range(2):
+            stage1_late(0, half)
         multiply(1, 0)
+        wo_banks = [transpose_chunk(alternate_blocks(wo_sb[:, 0, :]))]
         stage0(1, 0)
         stage1_early(1)
         multiply(1, 1)
-        wo_banks = [transpose_chunk(alternate_blocks(wo_sb[:, c, :])) for c in (0, 1)]
-        stages2to8(0)
+        wo_banks.append(transpose_chunk(alternate_blocks(wo_sb[:, 1, :])))
+        for half in range(2):
+            stages2to8(0, half)
         stage0(1, 1)
-        stage1_late(1)
-        stages2to8(1)
-        wo_banks.extend([transpose_chunk(alternate_blocks(wo_sb[:, c, :])) for c in (2, 3)])
+        wo_banks.append(transpose_chunk(alternate_blocks(wo_sb[:, 2, :])))
+        for half in range(2):
+            stage1_late(1, half)
+            stages2to8(1, half)
+        wo_banks.append(transpose_chunk(alternate_blocks(wo_sb[:, 3, :])))
 
         wo_grouped = keep.tile([P, PACK, PASSES, P, PACK], BF16, align_bytes=64)
         wo_codes = keep.tile([P, PACK, PASSES, P], U32, align_bytes=64)
@@ -315,28 +326,34 @@ def tile_butterflylayer_s_kernel(tc, x, w_in, w_out, b_out, a_pad, b_pad, out):
             regroup_chunk(wo_banks[c], wo_grouped[:, c])
             quantise_chunk(wo_grouped[:, c], wo_codes[:, c], wo_scales[:, c])
 
-        z0 = z_ps[0][:].rearrange("p t n -> p n t")
-        z1 = z_ps[1][:].rearrange("p t n -> p n t")
-        from_z0 = keep.tile([P, HALVES, BATCH, PACK], F32)
-        h_grouped = keep.tile([P, HALVES, BATCH, PACK], BF16, align_bytes=64)
+        from_z0 = keep.tile([P, HALVES, 2, BATCH // 2, PACK], F32)
+        h_grouped = keep.tile([P, HALVES, 2, BATCH // 2, PACK], BF16, align_bytes=64)
         h_codes = keep.tile([P, HALVES, BATCH], U32, align_bytes=64)
         h_scales = keep.tile([P, HALVES, BATCH], U8, align_bytes=64)
-        for g, of_z0, of_z1 in ((0, COS, SIN), (1, NEG_SIN, COS)):
-            nc.scalar.activation(
-                out=from_z0[:, g], in_=z0, func=COPY, scale=rot9(of_z0)
-            )
-            add_partner(h_grouped[:, g], z1, rot9(of_z1), from_z0[:, g])
+        from_z1 = ((0, SIN), (1, COS))
+        for g, of_z0 in ((0, COS), (1, NEG_SIN)):
+            for half in range(2):
+                nc.scalar.activation(
+                    out=from_z0[:, g, half],
+                    in_=z_ps[0, half][:].rearrange("p t n -> p n t"),
+                    func=COPY,
+                    scale=rot9(of_z0),
+                )
+        for half in range(2):
+            z1 = z_ps[1, half][:].rearrange("p t n -> p n t")
+            for g, of_z1 in from_z1:
+                add_partner(h_grouped[:, g, half], z1, rot9(of_z1), from_z0[:, g, half])
         for g in range(HALVES):
             nc.vector.quantize_mx(
                 out=h_codes[:, g, :].bitcast(FP8X4),
                 scales=h_scales[:, g, :],
-                in_=h_grouped[:, g].rearrange("p n j -> p (n j)"),
+                in_=h_grouped[:, g].rearrange("p h n j -> p (h n j)"),
             )
         for c in (2, 3):
             regroup_chunk(wo_banks[c], wo_grouped[:, c])
             quantise_chunk(wo_grouped[:, c], wo_codes[:, c], wo_scales[:, c])
 
-        out_ps = [fixed.tile([P, 2, P], F32, name="out_ps%d" % b, tag="piece%d" % (2 + b)) for b in range(2)]
+        out_ps = [fixed.tile([P, 2, P], F32, name="out_ps%d" % b, tag="piece%d" % b) for b in range(2)]
         out_sb = keep.tile([P, N_OUT], F32)
         for c in range(PACK):
             for g in range(HALVES):

from contextlib import ExitStack

import concourse.mybir as mybir
from concourse.masks import make_identity

F32 = mybir.dt.float32
BF16 = mybir.dt.bfloat16
U32 = mybir.dt.uint32
U8 = mybir.dt.uint8
I32 = mybir.dt.int32
FP8X4 = mybir.dt.float8_e4m3fn_x4
MULT = mybir.AluOpType.mult
ADD = mybir.AluOpType.add
COPY = mybir.ActivationFunctionType.Copy

P = 128
PACK = 4
K_PASS = P * PACK
BATCH = 128
K_IN = 1024
FEAT = 1024
N_OUT = 512
PASSES = K_IN // K_PASS
HALVES = FEAT // K_PASS
MID = 7
FIRST_MID = 2
LAST = 9
TAIL = LAST - FIRST_MID + 1
HALF_ROW = 64
COS, NEG_SIN, SIN = 0, 1, 2
ROT1, ROT9, ROT_END = 12, 18, 21

FLOPS = 2 * BATCH * K_IN * FEAT + 2 * BATCH * FEAT * N_OUT + 6 * BATCH * (FEAT // 2) * 10


def tile_butterflylayer_s_kernel(tc, x, w_in, w_out, b_out, a_pad, b_pad, out):
    nc = tc.nc
    with ExitStack() as ctx:
        keep = ctx.enter_context(tc.tile_pool(name="keep", bufs=1))
        ring = ctx.enter_context(tc.psum_pool(name="ring", bufs=4))
        fixed = ctx.enter_context(tc.psum_pool(name="fixed", bufs=1))
        ctx.enter_context(tc.manual_schedule())

        tab = keep.tile([P, 2, 3, HALF_ROW], BF16)
        nc.vector.memset(tab[:].bitcast(I32), 0)
        early = keep.tile([P, 2 * P], BF16)
        nc.vector.memset(early[:].bitcast(I32), 0)

        x_sb = keep.tile([P, K_IN], BF16)
        nc.sync.dma_start(out=x_sb[:], in_=x)
        w_sb = keep.tile([P, HALVES, PACK, K_IN], BF16)
        w_rows = w_in.rearrange("(g p t) k -> p g t k", g=HALVES, t=PACK)
        for g, quarters in ((0, slice(0, 2)), (0, slice(2, 4)), (1, slice(0, 2)), (1, slice(2, 3)), (1, slice(3, 4))):
            nc.sync.dma_start(out=w_sb[:, g, quarters, :], in_=w_rows[:, g, quarters, :])
            if g == 0 and quarters.start == 0:
                for piece, pad in ((0, a_pad), (1, b_pad), (2, a_pad)):
                    nc.sync.dma_start(
                        out=tab[0:TAIL, :, piece, :],
                        in_=pad[FIRST_MID : LAST + 1, 0:P].rearrange("l (h v) -> l h v", h=2),
                    )
                for row, pad in ((0, a_pad), (4, b_pad)):
                    nc.sync.dma_start(
                        out=early[row : row + 4, :],
                        in_=pad[0:FIRST_MID, :].rearrange("l (g c) -> (l g) c", g=2),
                    )
        wo_sb = keep.tile([P, PACK, FEAT], BF16)
        wo_rows = w_out.rearrange("(c r) k -> r c k", c=PACK)
        for c in range(0, PACK, 2):
            nc.sync.dma_start(out=wo_sb[:, c : c + 2, :], in_=wo_rows[:, c : c + 2, :])
        bias = keep.tile([P, N_OUT], BF16)
        nc.sync.dma_start(out=bias[:], in_=b_out.partition_broadcast(P))

        ident = keep.tile([P, P], F32)
        make_identity(nc, ident[:])
        ident_bf = keep.tile([P, P], BF16)
        nc.vector.tensor_copy(out=ident_bf[:], in_=ident[:])
        sign = keep.tile([P, 2, 2, TAIL], F32)
        nc.vector.memset(sign[:], 1.0)
        nc.vector.memset(sign[0:HALF_ROW, :, 1, :], -1.0)
        factor = keep.tile([P, HALVES, MID + 1, 2], F32)
        nc.vector.memset(factor[:], 1.0)

        def neighbouring_blocks(rows):
            words = rows.bitcast(F32)
            return [words[:, b * P : (b + 1) * P] for b in range(2 * PASSES)]

        def alternate_blocks(rows):
            words = rows.bitcast(F32)
            half = K_PASS // 2
            return [
                words[:, c * half + u : (c + 1) * half : 2] for c in range(PASSES) for u in range(2)
            ]

        def transpose_chunk(word_blocks):
            bank = ring.tile([P, 2 * PASSES, P], F32, name="bank")
            for b in range(2 * PASSES):
                nc.tensor.transpose(bank[:, b, :], word_blocks[b], ident[:])
            return bank

        def regroup_chunk(bank, grouped):
            nc.scalar.copy(
                out=grouped.bitcast(F32), in_=bank[:].rearrange("p (c u) r -> p c r u", u=2)
            )

        def quantise_chunk(grouped, codes, scales):
            nc.vector.quantize_mx(
                out=codes.rearrange("p c r -> p (c r)").bitcast(FP8X4),
                scales=scales.rearrange("p c r -> p (c r)"),
                in_=grouped.rearrange("p c r j -> p (c r j)"),
            )

        pick = keep.tile([P, 3, 4], BF16)
        nc.vector.tensor_copy(out=pick[:, COS, :], in_=ident[:, 0:4])
        nc.vector.tensor_scalar_mul(out=pick[:, NEG_SIN, :], in0=ident[:, 4:8], scalar1=-1.0)
        nc.vector.tensor_copy(out=pick[:, SIN, :], in_=ident[:, 4:8])

        spread = keep.tile([P, MID, HALVES * P], BF16)
        for m in (0, 1, 2, 3, 4, 5, 6):
            entries = min(P >> m, HALF_ROW)
            repeat = 1 << m
            src = ident_bf[:].rearrange("p (e v) -> p v e", e=2)[:, 0:entries, :].unsqueeze(3)
            src = src.to_broadcast([P, entries, 2, repeat])
            dst = spread[:, m, 0 : entries * 2 * repeat].rearrange("p (v e w) -> p v e w", e=2, w=repeat)
            if m in (2, 4, 6):
                nc.gpsimd.tensor_scalar(out=dst, in0=src, scalar1=1.0, scalar2=0.0, op0=MULT, op1=ADD)
            else:
                nc.vector.tensor_copy(out=dst, in_=src)

        x_grouped = keep.tile([P, PASSES, BATCH, PACK], BF16, align_bytes=64)
        x_codes = keep.tile([P, PASSES, BATCH], U32, align_bytes=64)
        x_scales = keep.tile([P, PASSES, BATCH], U8, align_bytes=64)
        w_grouped = keep.tile([P, HALVES, PACK, PASSES, P, PACK], BF16, align_bytes=64)
        w_codes = keep.tile([P, HALVES, PACK, PASSES, P], U32, align_bytes=64)
        w_scales = keep.tile([P, HALVES, PACK, PASSES, P], U8, align_bytes=64)
        h_ps = {}

        def transpose_piece(g, u):
            return [transpose_chunk(neighbouring_blocks(w_sb[:, g, t, :])) for t in (2 * u, 2 * u + 1)]

        def quantise_piece(g, u, banks):
            for e in range(2):
                t = 2 * u + e
                regroup_chunk(banks[e], w_grouped[:, g, t])
                quantise_chunk(w_grouped[:, g, t], w_codes[:, g, t], w_scales[:, g, t])

        def multiply(g, u):
            h_ps[g, u] = fixed.tile([P, 2, BATCH], F32, name="h%d%d" % (g, u), tag="piece%d" % (2 * g + u))
            for e in range(2):
                for c in range(PASSES):
                    nc.tensor.matmul_mx(
                        out=h_ps[g, u][:, e, :],
                        lhsT=w_codes[:, g, 2 * u + e, c, :].bitcast(FP8X4),
                        lhsT_scale=w_scales[:, g, 2 * u + e, c, :],
                        rhs=x_codes[:, c, :].bitcast(FP8X4),
                        rhs_scale=x_scales[:, c, :],
                        start=(c == 0),
                        stop=(c == PASSES - 1),
                    )

        rot = keep.tile([P, ROT_END], F32)
        columns = keep.tile([P, 2, 2, TAIL], BF16)

        def build_columns():
            col_ps = fixed.tile([P, 2, 2, TAIL], F32, name="col_ps", tag="piece1")
            for h in range(2):
                for o in range(2):
                    nc.tensor.matmul(
                        out=col_ps[:, h, o, :],
                        lhsT=tab[:, h, o : o + 2, :].rearrange("p s v -> p (s v)"),
                        rhs=ident_bf[:, 0:TAIL],
                        start=True,
                        stop=True,
                    )
            nc.vector.tensor_tensor(out=columns[:], in0=col_ps[:], in1=sign[:], op=MULT)

        def build_rot():
            rot_ps = fixed.tile([P, ROT_END], F32, name="rot_ps", tag="piece2")
            for u in range(2):
                nc.tensor.matmul(
                    out=rot_ps[:, 6 * u : 6 * u + 6], lhsT=early[:, u::2], rhs=pick[:, :, 0:2], start=True, stop=True
                )
            for g in range(HALVES):
                nc.tensor.matmul(
                    out=rot_ps[:, ROT1 + 3 * g : ROT1 + 3 * g + 3],
                    lhsT=early[:, g * P : (g + 1) * P],
                    rhs=pick[:, :, 2],
                    start=True,
                    stop=True,
                )
            for row, first, count in ((0, COS, 2), (HALF_ROW, SIN, 1)):
                nc.tensor.matmul(
                    out=rot_ps[:, ROT9 + first : ROT9 + first + count],
                    lhsT=ident_bf[:, row : row + 1].to_broadcast([P, P]),
                    rhs=columns[:, 0, 0:count, TAIL - 1],
                    start=True,
                    stop=True,
                )
            nc.vector.tensor_copy(out=rot[:], in_=rot_ps[:])

        def outer(groups, high, low, tables):
            wider = keep.tile([P, groups, high, low], F32, name="outer%d" % low)
            two = tables.rearrange("p (k two) w -> p k two w", two=2)
            nc.gpsimd.tensor_tensor(
                out=wider[:],
                in0=two[:, :, 1, 0:high].unsqueeze(3).to_broadcast([P, groups, high, low]),
                in1=two[:, :, 0, :].unsqueeze(2).to_broadcast([P, groups, high, low]),
                op=MULT,
            )
            return wider[:].rearrange("p k a b -> p k (a b)")

        def build_mid():
            factor_ps = fixed.tile([P, HALVES, MID, 2], F32, name="factor_ps", tag="piece3")
            for g in range(HALVES):
                for m in range(MID):
                    h, first = (g, 0) if m == 0 else (0, g * P)
                    nc.tensor.matmul(
                        out=factor_ps[:, g, m, :],
                        lhsT=spread[:, m, first : first + P],
                        rhs=columns[:, h, :, m],
                        start=True,
                        stop=True,
                    )
            nc.vector.tensor_copy(out=factor[:, :, 0:MID, :], in_=factor_ps[:])
            bits2 = outer(HALVES * 4, 2, 2, factor[:].rearrange("p g m o -> p (g m) o"))
            bits4 = outer(HALVES * 2, 4, 4, bits2)
            return outer(HALVES, 8, 16, bits4)

        def rot0(g, u, kind):
            return rot[:, 6 * u + 2 * kind + g : 6 * u + 2 * kind + g + 1]

        def rot1(g, kind):
            return rot[:, ROT1 + 3 * g + kind : ROT1 + 3 * g + kind + 1]

        def rot9(kind):
            return rot[:, ROT9 + kind : ROT9 + kind + 1]

        def add_partner(dst, partner, sine, scaled):
            nc.vector.scalar_tensor_tensor(out=dst, in0=partner, scalar=sine, in1=scaled, op0=MULT, op1=ADD)

        cos_h = keep.tile([P, HALVES, PACK, BATCH], F32)
        after0 = keep.tile([P, HALVES, PACK, BATCH], F32)
        share1 = keep.tile([P, HALVES, 2, 2, BATCH], F32)
        after1 = keep.tile([P, HALVES, 2, PACK, BATCH // 2], F32)
        LOW, HIGH = slice(0, 2), slice(2, 4)

        def stage0(g, u):
            h = h_ps[g, u]
            nc.scalar.activation(
                out=cos_h[:, g, 2 * u : 2 * u + 2, :], in_=h[:], func=COPY, scale=rot0(g, u, COS)
            )
            add_partner(after0[:, g, 2 * u, :], h[:, 1, :], rot0(g, u, SIN), cos_h[:, g, 2 * u, :])
            add_partner(after0[:, g, 2 * u + 1, :], h[:, 0, :], rot0(g, u, NEG_SIN), cos_h[:, g, 2 * u + 1, :])

        def stage1_early(g):
            for k, kind in ((0, COS), (1, NEG_SIN)):
                nc.vector.tensor_scalar_mul(
                    out=share1[:, g, k], in0=after0[:, g, LOW, :], scalar1=rot1(g, kind)
                )

        def stage1_late(g, half):
            batch = slice(half * (BATCH // 2), (half + 1) * (BATCH // 2))
            for k, (quarters, kind) in enumerate(((LOW, SIN), (HIGH, COS))):
                add_partner(
                    after1[:, g, half, quarters, :],
                    after0[:, g, HIGH, batch],
                    rot1(g, kind),
                    share1[:, g, k, :, batch],
                )

        z_ps = {}

        def stages2to8(g, half):
            z_ps[g, half] = fixed.tile(
                [P, PACK, BATCH // 2], F32, name="z%d_%d" % (g, half), tag="piece%d" % (2 * g + half)
            )
            nc.tensor.matmul(
                out=z_ps[g, half][:].rearrange("p t n -> p (t n)"),
                lhsT=mid[:, g, :],
                rhs=after1[:, g, half].rearrange("p t n -> p (t n)"),
                start=True,
                stop=True,
            )

        for warm_up in range(3):
            transpose_chunk([ident[:]] * 4)
        x_bank = transpose_chunk(neighbouring_blocks(x_sb[:]))
        banks = {(0, 0): transpose_piece(0, 0)}
        build_columns()
        regroup_chunk(x_bank, x_grouped[:])
        quantise_chunk(x_grouped[:], x_codes[:], x_scales[:])
        quantise_piece(0, 0, banks[0, 0])
        banks[0, 1] = transpose_piece(0, 1)
        build_rot()
        mid = build_mid()
        quantise_piece(0, 1, banks[0, 1])
        multiply(0, 0)
        stage0(0, 0)
        stage1_early(0)
        banks[1, 0] = transpose_piece(1, 0)
        quantise_piece(1, 0, banks[1, 0])
        multiply(0, 1)
        stage0(0, 1)
        banks[1, 1] = transpose_piece(1, 1)
        quantise_piece(1, 1, banks[1, 1])
        for half in range(2):
            stage1_late(0, half)
        multiply(1, 0)
        wo_banks = [transpose_chunk(alternate_blocks(wo_sb[:, 0, :]))]
        stage0(1, 0)
        stage1_early(1)
        multiply(1, 1)
        wo_banks.append(transpose_chunk(alternate_blocks(wo_sb[:, 1, :])))
        for half in range(2):
            stages2to8(0, half)
        stage0(1, 1)
        wo_banks.append(transpose_chunk(alternate_blocks(wo_sb[:, 2, :])))
        for half in range(2):
            stage1_late(1, half)
            stages2to8(1, half)
        wo_banks.append(transpose_chunk(alternate_blocks(wo_sb[:, 3, :])))

        wo_grouped = keep.tile([P, PACK, PASSES, P, PACK], BF16, align_bytes=64)
        wo_codes = keep.tile([P, PACK, PASSES, P], U32, align_bytes=64)
        wo_scales = keep.tile([P, PACK, PASSES, P], U8, align_bytes=64)
        for c in (0, 1):
            regroup_chunk(wo_banks[c], wo_grouped[:, c])
            quantise_chunk(wo_grouped[:, c], wo_codes[:, c], wo_scales[:, c])

        from_z0 = keep.tile([P, HALVES, 2, BATCH // 2, PACK], F32)
        h_grouped = keep.tile([P, HALVES, 2, BATCH // 2, PACK], BF16, align_bytes=64)
        h_codes = keep.tile([P, HALVES, BATCH], U32, align_bytes=64)
        h_scales = keep.tile([P, HALVES, BATCH], U8, align_bytes=64)
        from_z1 = ((0, SIN), (1, COS))
        for g, of_z0 in ((0, COS), (1, NEG_SIN)):
            for half in range(2):
                nc.scalar.activation(
                    out=from_z0[:, g, half],
                    in_=z_ps[0, half][:].rearrange("p t n -> p n t"),
                    func=COPY,
                    scale=rot9(of_z0),
                )
        for half in range(2):
            z1 = z_ps[1, half][:].rearrange("p t n -> p n t")
            for g, of_z1 in from_z1:
                add_partner(h_grouped[:, g, half], z1, rot9(of_z1), from_z0[:, g, half])
        for g in range(HALVES):
            nc.vector.quantize_mx(
                out=h_codes[:, g, :].bitcast(FP8X4),
                scales=h_scales[:, g, :],
                in_=h_grouped[:, g].rearrange("p h n j -> p (h n j)"),
            )
        for c in (2, 3):
            regroup_chunk(wo_banks[c], wo_grouped[:, c])
            quantise_chunk(wo_grouped[:, c], wo_codes[:, c], wo_scales[:, c])

        out_ps = [fixed.tile([P, 2, P], F32, name="out_ps%d" % b, tag="piece%d" % b) for b in range(2)]
        out_sb = keep.tile([P, N_OUT], F32)
        for c in range(PACK):
            for g in range(HALVES):
                nc.tensor.matmul_mx(
                    out=out_ps[c // 2][:, c % 2, :],
                    lhsT=h_codes[:, g, :].bitcast(FP8X4),
                    lhsT_scale=h_scales[:, g, :],
                    rhs=wo_codes[:, c, g, :].bitcast(FP8X4),
                    rhs_scale=wo_scales[:, c, g, :],
                    start=(g == 0),
                    stop=(g == HALVES - 1),
                )
            if c % 2 == 1:
                cols = slice((c - 1) * P, (c + 1) * P)
                nc.vector.tensor_tensor(
                    out=out_sb[:, cols],
                    in0=out_ps[c // 2][:].rearrange("p c r -> p (c r)"),
                    in1=bias[:, cols],
                    op=ADD,
                )
                nc.sync.dma_start(out=out[:, cols], in_=out_sb[:, cols])
